import numpy as np
import ml_dtypes


def mxq(x, axis, fmt="e4m3"):
    dtype, down = {"e4m3": (ml_dtypes.float8_e4m3fn, 7), "e5m2": (ml_dtypes.float8_e5m2, 14)}[fmt]
    v = np.moveaxis(np.asarray(x, np.float32).astype(ml_dtypes.bfloat16).astype(np.float64), axis, -1)
    blocks = v.reshape(v.shape[:-1] + (-1, 32))
    amax = np.abs(blocks).max(-1, keepdims=True)
    byte = np.maximum(np.where(amax > 0, np.frexp(amax)[1] - 1 + 127, 0) - down, 1)
    scale = np.exp2(byte - 127.0)
    codes = (blocks / scale).astype(np.float32).astype(dtype).astype(np.float64)
    return np.moveaxis((codes * scale).reshape(v.shape), -1, axis)


WIDE = False


def mx_kscale(k):
    if not WIDE:
        return np.ones(k)
    levels = np.array([10, -10, 5, -5, 0])
    a = np.random.permutation(np.resize(levels, k // 512 * 4)).reshape(k // 512, 4)
    idx = np.arange(k)
    return np.exp2(a[idx // 512, idx % 128 // 32])


BF16 = ml_dtypes.bfloat16


def bf(x):
    return np.asarray(x, np.float32).astype(BF16)


def f64(x):
    return np.asarray(x).astype(np.float64)


B, N, L, M, F = 32, 4, 1024, 512, 64
EPS = 1e-8
KAPPA0 = -3.0


def softplus(v):
    return np.logaddexp(v, 0.0)


def sigmoid(v):
    return 1.0 / (1.0 + np.exp(-v))


def setup_inputs():
    e = np.log2(mx_kscale(L))
    keep = np.abs(e) == np.abs(e).min()
    k0 = softplus(KAPPA0)
    t = np.zeros(L)
    t[keep] = np.sort(np.random.uniform(0.0, 1.0, int(keep.sum())))
    off = k0 * (np.log(2.0) * 2.0 * np.abs(e) + np.random.uniform(0.0, 1.0, L))
    t = np.where(keep, t, np.where(e > 0, 1.0 + off, -off))[:, None]
    t_left = np.random.uniform(0.0, 1.0, (N, M)) * 0.8
    t_right = t_left + 0.05 + 0.15 * np.random.uniform(0.0, 1.0, (N, M))
    kappa = KAPPA0 + 0.3 * np.random.standard_normal((N, 1))
    tq = f64(bf(t))[:, 0]
    kq = softplus(f64(bf(kappa)))
    d = np.maximum(np.maximum(tq - 1.0, -tq), 0.0)
    g = np.where(d > 0.0, 0.5, 1.0) * np.exp(d[None, :] / kq)
    x_aug = np.random.standard_normal((B, N, L, F)) * 0.15 * np.sqrt(L) * g[None, :, :, None]
    return {"x_aug": bf(x_aug), "t": bf(t), "t_left": bf(t_left), "t_right": bf(t_right), "kappa": bf(kappa)}


def reference(x_aug, t, t_left, t_right, kappa):
    t = f64(t)
    k = softplus(f64(kappa))[None, :, None]
    tl = f64(t_left)[None, :, None, :]
    tr = f64(t_right)[None, :, None, :]
    alpha = sigmoid((tr - t) / k) * sigmoid((t - tl) / k)
    numerator = mxq(alpha[0], 1, "e4m3").transpose(0, 2, 1) @ mxq(f64(x_aug), 2, "e4m3")
    denominator = alpha.sum(axis=2)[..., None]
    return numerator / (denominator + EPS)

@@ -1,0 +1,345 @@
+from contextlib import ExitStack
+
+import concourse.mybir as mybir
+
+F32 = mybir.dt.float32
+BF16 = mybir.dt.bfloat16
+I32 = mybir.dt.int32
+U32 = mybir.dt.uint32
+U8 = mybir.dt.uint8
+FP8X4 = mybir.dt.float8_e4m3fn_x4
+ACT = mybir.ActivationFunctionType
+ALU = mybir.AluOpType
+AX = mybir.AxisListType
+
+B, N, L, M, F = 32, 4, 1024, 512, 64
+EPS = 1e-8
+P = 128
+PACK = 4
+K_PASS = P * PACK
+PASSES = L // K_PASS
+CJ = PASSES * PACK
+MT = M // P
+BG = 8
+NG = B // BG
+COLS = BG * F
+CHUNKS = N * NG
+PIECES = N * 4
+W = 17
+LOG2E = 1.4426950408889634
+LN2_HI = 0.693145751953125
+LN2_LO = 1.4286068203094173e-06
+
+LOAD_LEAD = 7
+SIG_LEAD = 6
+PROD_LEAD = 5
+XR_LEAD = 4
+XQ_LEAD = 3
+RAW_BUFS = 5
+
+FLOPS = 2 * B * N * M * L * F
+
+
+def tile_weightedaggregation_t_kernel(tc, x_aug, t, t_left, t_right, kappa, out):
+    nc = tc.nc
+    with ExitStack() as ctx:
+        const = ctx.enter_context(tc.tile_pool(name="const", bufs=1))
+        rawp = ctx.enter_context(tc.tile_pool(name="rawp", bufs=RAW_BUFS))
+        xgp = ctx.enter_context(tc.tile_pool(name="xgp", bufs=3))
+        xcp = ctx.enter_context(tc.tile_pool(name="xcp", bufs=4))
+        outp = ctx.enter_context(tc.tile_pool(name="outp", bufs=4))
+        sgp = ctx.enter_context(tc.tile_pool(name="sgp", bufs=3))
+        a32p = ctx.enter_context(tc.tile_pool(name="a32p", bufs=2))
+        gp = ctx.enter_context(tc.tile_pool(name="gp", bufs=2))
+        accp = ctx.enter_context(tc.psum_pool(name="accp", bufs=7))
+        denp = ctx.enter_context(tc.psum_pool(name="denp", bufs=1))
+        ctx.enter_context(tc.manual_schedule())
+
+        kap_bf = const.tile([P, N], BF16)
+        nc.sync.dma_start(out=kap_bf[:], in_=kappa.rearrange("n o -> (n o)").partition_broadcast(P))
+        tt_bf = const.tile([P, PASSES, PACK], BF16)
+        nc.sync.dma_start(out=tt_bf[:], in_=t.rearrange("(c p j) o -> p c (j o)", c=PASSES, j=PACK))
+        trb = const.tile([P, N, M], BF16)
+        nc.scalar.dma_start(out=trb[:].rearrange("p n m -> p (n m)"),
+                            in_=t_right.rearrange("n m -> (n m)").partition_broadcast(P))
+        tlb = const.tile([P, N, M], BF16)
+        nc.scalar.dma_start(out=tlb[:].rearrange("p n m -> p (n m)"),
+                            in_=t_left.rearrange("n m -> (n m)").partition_broadcast(P))
+
+        raws = {}
+        xgs = {}
+        xqs = {}
+        st = {}
+
+        def load(i):
+            n, g = divmod(i, NG)
+            raw = rawp.tile([P, PASSES, BG, PACK * F], BF16, name="raw")
+            for c in range(PASSES):
+                nc.sync.dma_start(
+                    out=raw[:, c],
+                    in_=x_aug[g * BG:(g + 1) * BG, n, c * K_PASS:(c + 1) * K_PASS, :].rearrange(
+                        "b (p j) f -> p b (j f)", j=PACK
+                    ),
+                )
+            raws[i] = raw
+
+        def regroup(i, on_scalar):
+            raw = raws[i]
+            if i not in xgs:
+                xg = xgp.tile([P, PASSES, COLS, PACK], BF16, name="xg", align_bytes=64)
+                xgs[i] = xg
+            xg = xgs[i]
+            for c in range(PASSES):
+                if (i, c) in S_REGROUP:
+                    if on_scalar:
+                        nc.scalar.copy(
+                            out=xg[:, c].rearrange("p (b f) j -> p b f j", b=BG),
+                            in_=raw[:, c].rearrange("p b (j f) -> p b f j", j=PACK),
+                        )
+                elif not on_scalar:
+                    nc.vector.tensor_copy(
+                        out=xg[:, c].rearrange("p (b g i) j -> p b g j i", b=BG, i=4),
+                        in_=raw[:, c].rearrange("p b (j g i) -> p b g j i", j=PACK, i=4),
+                    )
+
+        S_REGROUP = ((0, 0), (0, 1), (1, 0))
+
+        for i in range(2):
+            load(i)
+
+        ones = const.tile([P, 2], F32)
+        nc.vector.memset(ones[:], 1.0)
+        warm = const.tile([P, 2], F32)
+        nc.scalar.activation(out=warm[:], in_=ones[:], func=ACT.Sigmoid)
+        fact = const.tile([P, 2, W], F32)
+        fac = 1.0
+        for i in range(W):
+            nc.vector.memset(fact[:, 0, i:i + 1], fac)
+            nc.vector.memset(fact[:, 1, i:i + 1], float(2 * i + 1))
+            fac = fac * (i + 1)
+        coef = const.tile([P, 2, W], F32)
+        nc.vector.reciprocal(out=coef[:], in_=fact[:])
+        tp = const.tile([P, N, W], F32)
+        nc.vector.memset(tp[:], 1.0)
+        up = const.tile([P, N, W], F32)
+        nc.vector.memset(up[:], 1.0)
+
+        regroup(0, True)
+        regroup(1, True)
+
+        trp = const.tile([P, N, M], BF16)
+        tlp = const.tile([P, N, M], BF16)
+        for n in range(N):
+            for src, dst in ((trb, trp), (tlb, tlp)):
+                nc.gpsimd.tensor_scalar(
+                    out=dst[:, n, :].rearrange("p (j q) -> p j q", j=MT),
+                    in0=src[:, n, :].rearrange("p (q j) -> p j q", j=MT),
+                    scalar1=1.0, scalar2=0.0, op0=ALU.mult, op1=ALU.add,
+                )
+
+        def powers(pt):
+            nc.vector.tensor_tensor(out=pt[:, :, 2:3], in0=pt[:, :, 1:2], in1=pt[:, :, 1:2], op=ALU.mult)
+            for lo in (2, 4, 8):
+                nc.vector.tensor_tensor(
+                    out=pt[:, :, lo + 1:2 * lo + 1], in0=pt[:, :, 1:lo + 1],
+                    in1=pt[:, :, lo:lo + 1].to_broadcast([P, N, lo]), op=ALU.mult,
+                )
+
+        def series(pt, row, name):
+            powers(pt)
+            terms = const.tile([P, N, W], F32, name="terms_" + name)
+            nc.vector.tensor_tensor(out=terms[:], in0=pt[:], in1=coef[:, row:row + 1, :].to_broadcast([P, N, W]),
+                                    op=ALU.mult)
+            total = const.tile([P, N], F32, name="total_" + name)
+            nc.vector.tensor_reduce(out=total[:], in_=terms[:], axis=AX.X, op=ALU.add)
+            return total
+
+        kap = const.tile([P, N], F32)
+        nc.vector.tensor_copy(out=kap[:], in_=kap_bf[:])
+        tt = const.tile([P, CJ], F32)
+        nc.vector.tensor_copy(out=tt[:], in_=tt_bf[:].rearrange("p c j -> p (c j)"))
+        a0 = const.tile([P, N], F32)
+        nc.vector.scalar_tensor_tensor(out=a0[:], in0=kap[:], scalar=-1.0, in1=kap[:], op0=ALU.mult, op1=ALU.max)
+        aa = const.tile([P, N], F32)
+        nc.vector.tensor_scalar(out=aa[:], in0=a0[:], scalar1=80.0, scalar2=None, op0=ALU.min)
+        n_i = const.tile([P, N], I32)
+        nc.vector.tensor_scalar(out=n_i[:], in0=aa[:], scalar1=LOG2E, scalar2=None, op0=ALU.mult)
+        nfl = const.tile([P, N], F32)
+        nc.vector.tensor_copy(out=nfl[:], in_=n_i[:])
+        r1 = const.tile([P, N], F32)
+        nc.vector.scalar_tensor_tensor(out=r1[:], in0=nfl[:], scalar=LN2_HI, in1=aa[:], op0=ALU.mult, op1=ALU.subtract)
+        nc.vector.scalar_tensor_tensor(out=tp[:, :, 1], in0=nfl[:], scalar=LN2_LO, in1=r1[:], op0=ALU.mult, op1=ALU.add)
+        e_i = const.tile([P, N], I32)
+        nc.vector.tensor_scalar(out=e_i[:], in0=n_i[:], scalar1=-1.0, scalar2=127.0, op0=ALU.mult, op1=ALU.add)
+        p_i = const.tile([P, N], I32)
+        nc.vector.tensor_single_scalar(out=p_i[:], in_=e_i[:], scalar=23, op=ALU.logical_shift_left)
+        er = series(tp, 0, "exp")
+        yy = const.tile([P, N], F32)
+        nc.vector.tensor_tensor(out=yy[:], in0=er[:], in1=p_i[:].bitcast(F32), op=ALU.mult)
+        dd = const.tile([P, N], F32)
+        nc.vector.tensor_scalar(out=dd[:], in0=yy[:], scalar1=2.0, scalar2=None, op0=ALU.add)
+        rd = const.tile([P, N], F32)
+        nc.vector.reciprocal(out=rd[:], in_=dd[:])
+        ss = const.tile([P, N], F32)
+        nc.vector.tensor_tensor(out=ss[:], in0=yy[:], in1=rd[:], op=ALU.mult)
+        nc.vector.tensor_tensor(out=up[:, :, 1], in0=ss[:], in1=ss[:], op=ALU.mult)
+        pl = series(up, 1, "log")
+        l1p = const.tile([P, N], F32)
+        nc.vector.scalar_tensor_tensor(out=l1p[:], in0=pl[:], scalar=2.0, in1=ss[:], op0=ALU.mult, op1=ALU.mult)
+        kk = const.tile([P, N], F32)
+        nc.vector.scalar_tensor_tensor(out=kk[:], in0=kap[:], scalar=0.0, in1=l1p[:], op0=ALU.max, op1=ALU.add)
+        rk = const.tile([P, N], F32)
+        nc.vector.reciprocal(out=rk[:], in_=kk[:])
+        nrk = const.tile([P, N], F32)
+        nc.vector.tensor_scalar(out=nrk[:], in0=rk[:], scalar1=-1.0, scalar2=None, op0=ALU.mult)
+
+        bt = const.tile([P, N, CJ], F32)
+        nc.vector.tensor_tensor(out=bt[:], in0=tt[:].unsqueeze(1).to_broadcast([P, N, CJ]),
+                                in1=rk[:].unsqueeze(2).to_broadcast([P, N, CJ]), op=ALU.mult)
+        nbt = const.tile([P, N, CJ], F32)
+        nc.vector.tensor_scalar(out=nbt[:], in0=bt[:], scalar1=-1.0, scalar2=None, op0=ALU.mult)
+
+        rden = const.tile([P, N, MT], F32)
+        a_codes = []
+        a_scales = []
+        for n in range(N):
+            ac = const.tile([P, PASSES, M], U32, name="ac%d" % n, align_bytes=64)
+            asc = const.tile([P, PASSES, M], U8, name="as%d" % n, align_bytes=64)
+            a_codes.append(ac)
+            a_scales.append(asc)
+
+        def sig(q):
+            n, g = divmod(q, 4)
+            c, h = divmod(g, 2)
+            s1 = sgp.tile([P, 2, M], F32, name="s1")
+            s2 = sgp.tile([P, 2, M], F32, name="s2")
+            for e in range(2):
+                cj = c * PACK + 2 * h + e
+                nc.scalar.activation(out=s1[:, e, :], in_=trp[:, n, :], func=ACT.Sigmoid,
+                                     bias=nbt[:, n, cj:cj + 1], scale=rk[:, n:n + 1])
+                nc.scalar.activation(out=s2[:, e, :], in_=tlp[:, n, :], func=ACT.Sigmoid,
+                                     bias=bt[:, n, cj:cj + 1], scale=nrk[:, n:n + 1])
+            st[("s", q)] = (s1, s2)
+
+        def prod(q):
+            h = q % 2
+            if h == 0:
+                a32 = a32p.tile([P, PACK, M], F32, name="a32")
+                st[("a", q // 2)] = a32
+            a32 = st[("a", q // 2)]
+            s1, s2 = st[("s", q)]
+            nc.vector.tensor_tensor(out=a32[:, 2 * h:2 * h + 2, :], in0=s1[:], in1=s2[:], op=ALU.mult)
+
+        def conv(half, on_scalar):
+            a32 = st[("a", half)]
+            grp = gp.tile([P, M, PACK], BF16, name="grp", align_bytes=64)
+            if on_scalar:
+                nc.scalar.copy(out=grp[:], in_=a32[:].rearrange("p j w -> p w j"))
+            else:
+                nc.vector.tensor_copy(out=grp[:], in_=a32[:].rearrange("p j w -> p w j"))
+            st[("g", half)] = grp
+
+        def qa(half):
+            n, c = divmod(half, 2)
+            nc.vector.quantize_mx(
+                out=a_codes[n][:, c, :].bitcast(FP8X4),
+                scales=a_scales[n][:, c, :],
+                in_=st[("g", half)][:].rearrange("p w j -> p (w j)"),
+            )
+
+        def den(half):
+            n, c = divmod(half, 2)
+            if c == 0:
+                den_ps = denp.tile([P, PASSES, MT, 2], F32, name="den_ps")
+                st[("d", n)] = den_ps
+            a32 = st[("a", half)]
+            for mt in range(MT):
+                for j in range(PACK):
+                    nc.tensor.matmul(
+                        out=st[("d", n)][:, c, mt, :],
+                        lhsT=a32[:, j, mt * P:(mt + 1) * P],
+                        rhs=ones[:],
+                        start=(j == 0), stop=(j == PACK - 1),
+                    )
+
+        def rden_of(n):
+            dsum = const.tile([P, MT], F32, name="dsum%d" % n)
+            nc.vector.tensor_reduce(
+                out=dsum[:], in_=st[("d", n)][:, :, :, 0].rearrange("p c m -> p m c"), axis=AX.X, op=ALU.add
+            )
+            dse = const.tile([P, MT], F32, name="dse%d" % n)
+            nc.vector.tensor_scalar(out=dse[:], in0=dsum[:], scalar1=EPS, scalar2=None, op0=ALU.add)
+            nc.vector.reciprocal(out=rden[:, n, :], in_=dse[:])
+
+        def quant(i):
+            xg = xgs[i]
+            xc = xcp.tile([P, PASSES, COLS], U32, name="xc", align_bytes=64)
+            xs = xcp.tile([P, PASSES, COLS], U8, name="xs", align_bytes=64)
+            nc.vector.quantize_mx(
+                out=xc[:].rearrange("p c w -> p (c w)").bitcast(FP8X4),
+                scales=xs[:].rearrange("p c w -> p (c w)"),
+                in_=xg[:].rearrange("p c w j -> p (c w j)"),
+            )
+            xqs[i] = (xc, xs)
+
+        def multiply(i):
+            n, g = divmod(i, NG)
+            xc, xs = xqs[i]
+            o_sb = outp.tile([P, BG, MT, F], F32, name="o_sb")
+            for mt in range(MT):
+                acc = accp.tile([P, COLS], F32, name="acc")
+                for c in range(PASSES):
+                    nc.tensor.matmul_mx(
+                        out=acc[:],
+                        lhsT=a_codes[n][:, c, mt * P:(mt + 1) * P].bitcast(FP8X4),
+                        lhsT_scale=a_scales[n][:, c, mt * P:(mt + 1) * P],
+                        rhs=xc[:, c, :].bitcast(FP8X4),
+                        rhs_scale=xs[:, c, :],
+                        start=(c == 0), stop=(c == PASSES - 1),
+                    )
+                if i >= CHUNKS - 3 and mt % 2 == 1:
+                    nc.vector.tensor_scalar(
+                        out=o_sb[:, :, mt, :], in0=acc[:].rearrange("p (b f) -> p b f", f=F),
+                        scalar1=rden[:, n, mt:mt + 1], scalar2=None, op0=ALU.mult,
+                    )
+                else:
+                    nc.scalar.activation(
+                        out=o_sb[:, :, mt, :], in_=acc[:].rearrange("p (b f) -> p b f", f=F),
+                        func=ACT.Copy, scale=rden[:, n, mt:mt + 1],
+                    )
+            nc.sync.dma_start(
+                out=out[g * BG:(g + 1) * BG, n, :, :].rearrange("b (p m) f -> p b (m f)", m=MT),
+                in_=o_sb[:].rearrange("p b m f -> p b (m f)"),
+            )
+
+        def s_conv(half):
+            return half >= 2 and half % 2 == 0
+
+        for p in range(-SIG_LEAD, CHUNKS):
+            if 2 <= p + LOAD_LEAD < CHUNKS:
+                load(p + LOAD_LEAD)
+            if 0 <= p + SIG_LEAD < PIECES:
+                sig(p + SIG_LEAD)
+            qprev = p - 1 + PROD_LEAD
+            if 0 <= qprev < PIECES and qprev % 2 == 1 and s_conv(qprev // 2):
+                conv(qprev // 2, True)
+            if p >= 0:
+                multiply(p)
+            q = p + PROD_LEAD
+            if 0 <= qprev < PIECES and qprev % 4 == 3:
+                rden_of(qprev // 4)
+            if 0 <= q < PIECES:
+                prod(q)
+            if 0 <= p + XQ_LEAD < CHUNKS:
+                quant(p + XQ_LEAD)
+            v_fin = 0 <= q < PIECES and q % 2 == 1 and not s_conv(q // 2)
+            if v_fin:
+                conv(q // 2, False)
+            if 0 <= p + XR_LEAD < CHUNKS:
+                regroup(p + XR_LEAD, False)
+            if v_fin:
+                qa(q // 2)
+            if 0 <= qprev < PIECES and qprev % 2 == 1 and s_conv(qprev // 2):
+                qa(qprev // 2)
+            if 0 <= q < PIECES and q % 2 == 1:
+                den(q // 2)

@@ -36,6 +36,7 @@ PROD_LEAD = 5
 XR_LEAD = 4
 XQ_LEAD = 3
 RAW_BUFS = 5
+RUNS = 4
 
 FLOPS = 2 * B * N * M * L * F
 
@@ -75,12 +76,14 @@ def tile_weightedaggregation_t_kernel(tc, x_aug, t, t_left, t_right, kappa, out)
             n, g = divmod(i, NG)
             raw = rawp.tile([P, PASSES, BG, PACK * F], BF16, name="raw")
             for c in range(PASSES):
-                nc.sync.dma_start(
-                    out=raw[:, c],
-                    in_=x_aug[g * BG:(g + 1) * BG, n, c * K_PASS:(c + 1) * K_PASS, :].rearrange(
-                        "b (p j) f -> p b (j f)", j=PACK
-                    ),
-                )
+                for bh in range(BG // RUNS):
+                    b0 = g * BG + bh * RUNS
+                    nc.sync.dma_start(
+                        out=raw[:, c, bh * RUNS:(bh + 1) * RUNS, :],
+                        in_=x_aug[b0:b0 + RUNS, n, c * K_PASS:(c + 1) * K_PASS, :].rearrange(
+                            "b (p j) f -> p b (j f)", j=PACK
+                        ),
+                    )
             raws[i] = raw
 
         def regroup(i, on_scalar):
@@ -307,10 +310,12 @@ def tile_weightedaggregation_t_kernel(tc, x_aug, t, t_left, t_right, kappa, out)
                         out=o_sb[:, :, mt, :], in_=acc[:].rearrange("p (b f) -> p b f", f=F),
                         func=ACT.Copy, scale=rden[:, n, mt:mt + 1],
                     )
-            nc.sync.dma_start(
-                out=out[g * BG:(g + 1) * BG, n, :, :].rearrange("b (p m) f -> p b (m f)", m=MT),
-                in_=o_sb[:].rearrange("p b m f -> p b (m f)"),
-            )
+            for bh in range(BG // RUNS):
+                b0 = g * BG + bh * RUNS
+                nc.scalar.dma_start(
+                    out=out[b0:b0 + RUNS, n, :, :].rearrange("b (p m) f -> p b (m f)", m=MT),
+                    in_=o_sb[:, bh * RUNS:(bh + 1) * RUNS].rearrange("p b m f -> p b (m f)"),
+                )
 
         def s_conv(half):
             return half >= 2 and half % 2 == 0

@@ -31,8 +31,8 @@ LN2_HI = 0.693145751953125
 LN2_LO = 1.4286068203094173e-06
 
 LOAD_LEAD = 7
-SIG_LEAD = 6
-PROD_LEAD = 5
+SIG_LEAD = 7
+PROD_LEAD = 6
 XR_LEAD = 4
 XQ_LEAD = 3
 RAW_BUFS = 5
@@ -50,7 +50,7 @@ def tile_weightedaggregation_t_kernel(tc, x_aug, t, t_left, t_right, kappa, out)
         xcp = ctx.enter_context(tc.tile_pool(name="xcp", bufs=4))
         outp = ctx.enter_context(tc.tile_pool(name="outp", bufs=4))
         sgp = ctx.enter_context(tc.tile_pool(name="sgp", bufs=3))
-        a32p = ctx.enter_context(tc.tile_pool(name="a32p", bufs=2))
+        a32p = ctx.enter_context(tc.tile_pool(name="a32p", bufs=3))
         gp = ctx.enter_context(tc.tile_pool(name="gp", bufs=2))
         accp = ctx.enter_context(tc.psum_pool(name="accp", bufs=7))
         denp = ctx.enter_context(tc.psum_pool(name="denp", bufs=1))
@@ -250,20 +250,19 @@ def tile_weightedaggregation_t_kernel(tc, x_aug, t, t_left, t_right, kappa, out)
                 in_=st[("g", half)][:].rearrange("p w j -> p (w j)"),
             )
 
-        def den(half):
+        def den(half, mt):
             n, c = divmod(half, 2)
-            if c == 0:
+            if c == 0 and mt == 0:
                 den_ps = denp.tile([P, PASSES, MT, 2], F32, name="den_ps")
                 st[("d", n)] = den_ps
             a32 = st[("a", half)]
-            for mt in range(MT):
-                for j in range(PACK):
-                    nc.tensor.matmul(
-                        out=st[("d", n)][:, c, mt, :],
-                        lhsT=a32[:, j, mt * P:(mt + 1) * P],
-                        rhs=ones[:],
-                        start=(j == 0), stop=(j == PACK - 1),
-                    )
+            for j in range(PACK):
+                nc.tensor.matmul(
+                    out=st[("d", n)][:, c, mt, :],
+                    lhsT=a32[:, j, mt * P:(mt + 1) * P],
+                    rhs=ones[:],
+                    start=(j == 0), stop=(j == PACK - 1),
+                )
 
         def rden_of(n):
             dsum = const.tile([P, MT], F32, name="dsum%d" % n)
@@ -285,7 +284,7 @@ def tile_weightedaggregation_t_kernel(tc, x_aug, t, t_left, t_right, kappa, out)
             )
             xqs[i] = (xc, xs)
 
-        def multiply(i):
+        def multiply(i, den_half):
             n, g = divmod(i, NG)
             xc, xs = xqs[i]
             o_sb = outp.tile([P, BG, MT, F], F32, name="o_sb")
@@ -300,6 +299,8 @@ def tile_weightedaggregation_t_kernel(tc, x_aug, t, t_left, t_right, kappa, out)
                         rhs_scale=xs[:, c, :],
                         start=(c == 0), stop=(c == PASSES - 1),
                     )
+                if den_half is not None:
+                    den(den_half, mt)
                 if i >= CHUNKS - 3 and mt % 2 == 1:
                     nc.vector.tensor_scalar(
                         out=o_sb[:, :, mt, :], in0=acc[:].rearrange("p (b f) -> p b f", f=F),
@@ -328,11 +329,16 @@ def tile_weightedaggregation_t_kernel(tc, x_aug, t, t_left, t_right, kappa, out)
             qprev = p - 1 + PROD_LEAD
             if 0 <= qprev < PIECES and qprev % 2 == 1 and s_conv(qprev // 2):
                 conv(qprev // 2, True)
+            den_half = qprev // 2 if (0 <= qprev < PIECES and qprev % 2 == 1) else None
             if p >= 0:
-                multiply(p)
+                multiply(p, den_half)
+            elif den_half is not None:
+                for mt in range(MT):
+                    den(den_half, mt)
             q = p + PROD_LEAD
-            if 0 <= qprev < PIECES and qprev % 4 == 3:
-                rden_of(qprev // 4)
+            qpp = qprev - 1
+            if 0 <= qpp < PIECES and qpp % 4 == 3:
+                rden_of(qpp // 4)
             if 0 <= q < PIECES:
                 prod(q)
             if 0 <= p + XQ_LEAD < CHUNKS:
@@ -346,5 +352,3 @@ def tile_weightedaggregation_t_kernel(tc, x_aug, t, t_left, t_right, kappa, out)
                 qa(q // 2)
             if 0 <= qprev < PIECES and qprev % 2 == 1 and s_conv(qprev // 2):
                 qa(qprev // 2)
-            if 0 <= q < PIECES and q % 2 == 1:
-                den(q // 2)

@@ -1,6 +1,7 @@
 from contextlib import ExitStack
 
 import concourse.mybir as mybir
+from concourse.masks import make_identity
 
 F32 = mybir.dt.float32
 BF16 = mybir.dt.bfloat16
@@ -31,8 +32,8 @@ LN2_HI = 0.693145751953125
 LN2_LO = 1.4286068203094173e-06
 
 LOAD_LEAD = 7
-SIG_LEAD = 7
-PROD_LEAD = 6
+SIG_LEAD = 8
+PROD_LEAD = 7
 XR_LEAD = 4
 XQ_LEAD = 3
 RAW_BUFS = 5
@@ -52,8 +53,8 @@ def tile_weightedaggregation_t_kernel(tc, x_aug, t, t_left, t_right, kappa, out)
         sgp = ctx.enter_context(tc.tile_pool(name="sgp", bufs=3))
         a32p = ctx.enter_context(tc.tile_pool(name="a32p", bufs=3))
         gp = ctx.enter_context(tc.tile_pool(name="gp", bufs=2))
-        accp = ctx.enter_context(tc.psum_pool(name="accp", bufs=7))
-        denp = ctx.enter_context(tc.psum_pool(name="denp", bufs=1))
+        accp = ctx.enter_context(tc.psum_pool(name="accp", bufs=6))
+        denp = ctx.enter_context(tc.psum_pool(name="denp", bufs=2))
         ctx.enter_context(tc.manual_schedule())
 
         kap_bf = const.tile([P, N], BF16)
@@ -92,26 +93,28 @@ def tile_weightedaggregation_t_kernel(tc, x_aug, t, t_left, t_right, kappa, out)
                 xg = xgp.tile([P, PASSES, COLS, PACK], BF16, name="xg", align_bytes=64)
                 xgs[i] = xg
             xg = xgs[i]
-            for c in range(PASSES):
-                if (i, c) in S_REGROUP:
-                    if on_scalar:
+            if i in S_REGROUP:
+                if on_scalar:
+                    for c in range(PASSES):
                         nc.scalar.copy(
                             out=xg[:, c].rearrange("p (b f) j -> p b f j", b=BG),
                             in_=raw[:, c].rearrange("p b (j f) -> p b f j", j=PACK),
                         )
-                elif not on_scalar:
-                    nc.vector.tensor_copy(
-                        out=xg[:, c].rearrange("p (b g i) j -> p b g j i", b=BG, i=4),
-                        in_=raw[:, c].rearrange("p b (j g i) -> p b g j i", j=PACK, i=4),
-                    )
+            elif not on_scalar:
+                nc.vector.tensor_copy(
+                    out=xg[:].rearrange("p c (b g i) j -> p (c b) g j i", b=BG, i=4),
+                    in_=raw[:].rearrange("p c b (j g i) -> p (c b) g j i", j=PACK, i=4),
+                )
 
-        S_REGROUP = ((0, 0), (0, 1), (1, 0))
+        S_REGROUP = (0,)
 
-        for i in range(2):
+        for i in range(RAW_BUFS):
             load(i)
 
         ones = const.tile([P, 2], F32)
         nc.vector.memset(ones[:], 1.0)
+        ident = const.tile([P, P], F32)
+        make_identity(nc, ident[:])
         warm = const.tile([P, 2], F32)
         nc.scalar.activation(out=warm[:], in_=ones[:], func=ACT.Sigmoid)
         fact = const.tile([P, 2, W], F32)
@@ -128,7 +131,6 @@ def tile_weightedaggregation_t_kernel(tc, x_aug, t, t_left, t_right, kappa, out)
         nc.vector.memset(up[:], 1.0)
 
         regroup(0, True)
-        regroup(1, True)
 
         trp = const.tile([P, N, M], BF16)
         tlp = const.tile([P, N, M], BF16)
@@ -250,25 +252,23 @@ def tile_weightedaggregation_t_kernel(tc, x_aug, t, t_left, t_right, kappa, out)
                 in_=st[("g", half)][:].rearrange("p w j -> p (w j)"),
             )
 
-        def den(half, mt):
-            n, c = divmod(half, 2)
-            if c == 0 and mt == 0:
-                den_ps = denp.tile([P, PASSES, MT, 2], F32, name="den_ps")
-                st[("d", n)] = den_ps
-            a32 = st[("a", half)]
-            for j in range(PACK):
-                nc.tensor.matmul(
-                    out=st[("d", n)][:, c, mt, :],
-                    lhsT=a32[:, j, mt * P:(mt + 1) * P],
-                    rhs=ones[:],
-                    start=(j == 0), stop=(j == PACK - 1),
-                )
+        def den(n):
+            den_ps = denp.tile([P, MT, P], F32, name="den_ps")
+            st[("d", n)] = den_ps
+            for mt in range(MT):
+                for cj in range(CJ):
+                    c, j = divmod(cj, PACK)
+                    nc.tensor.matmul(
+                        out=den_ps[:, mt, :],
+                        lhsT=st[("a", 2 * n + c)][:, j, mt * P:(mt + 1) * P],
+                        rhs=ident[:],
+                        is_transpose=True,
+                        start=(cj == 0), stop=(cj == CJ - 1),
+                    )
 
         def rden_of(n):
             dsum = const.tile([P, MT], F32, name="dsum%d" % n)
-            nc.vector.tensor_reduce(
-                out=dsum[:], in_=st[("d", n)][:, :, :, 0].rearrange("p c m -> p m c"), axis=AX.X, op=ALU.add
-            )
+            nc.vector.tensor_reduce(out=dsum[:], in_=st[("d", n)][:], axis=AX.X, op=ALU.add)
             dse = const.tile([P, MT], F32, name="dse%d" % n)
             nc.vector.tensor_scalar(out=dse[:], in0=dsum[:], scalar1=EPS, scalar2=None, op0=ALU.add)
             nc.vector.reciprocal(out=rden[:, n, :], in_=dse[:])
@@ -284,12 +284,29 @@ def tile_weightedaggregation_t_kernel(tc, x_aug, t, t_left, t_right, kappa, out)
             )
             xqs[i] = (xc, xs)
 
-        def multiply(i, den_half):
+        def evacuate(on_vector, dst, src, n, mt):
+            if on_vector:
+                nc.vector.tensor_scalar(out=dst, in0=src, scalar1=rden[:, n, mt:mt + 1], scalar2=None, op0=ALU.mult)
+            else:
+                nc.scalar.activation(out=dst, in_=src, func=ACT.Copy, scale=rden[:, n, mt:mt + 1])
+
+        def store(i, o_sb, bh):
+            n, g = divmod(i, NG)
+            b0 = g * BG + bh * RUNS
+            nc.scalar.dma_start(
+                out=out[b0:b0 + RUNS, n, :, :].rearrange("b (p m) f -> p b (m f)", m=MT),
+                in_=o_sb[:, bh * RUNS:(bh + 1) * RUNS].rearrange("p b m f -> p b (m f)"),
+            )
+
+        def multiply(i):
             n, g = divmod(i, NG)
             xc, xs = xqs[i]
             o_sb = outp.tile([P, BG, MT, F], F32, name="o_sb")
+            last = i == CHUNKS - 1
+            accs = []
             for mt in range(MT):
                 acc = accp.tile([P, COLS], F32, name="acc")
+                accs.append(acc)
                 for c in range(PASSES):
                     nc.tensor.matmul_mx(
                         out=acc[:],
@@ -299,56 +316,68 @@ def tile_weightedaggregation_t_kernel(tc, x_aug, t, t_left, t_right, kappa, out)
                         rhs_scale=xs[:, c, :],
                         start=(c == 0), stop=(c == PASSES - 1),
                     )
-                if den_half is not None:
-                    den(den_half, mt)
-                if i >= CHUNKS - 3 and mt % 2 == 1:
-                    nc.vector.tensor_scalar(
-                        out=o_sb[:, :, mt, :], in0=acc[:].rearrange("p (b f) -> p b f", f=F),
-                        scalar1=rden[:, n, mt:mt + 1], scalar2=None, op0=ALU.mult,
-                    )
-                else:
-                    nc.scalar.activation(
-                        out=o_sb[:, :, mt, :], in_=acc[:].rearrange("p (b f) -> p b f", f=F),
-                        func=ACT.Copy, scale=rden[:, n, mt:mt + 1],
-                    )
-            for bh in range(BG // RUNS):
-                b0 = g * BG + bh * RUNS
-                nc.scalar.dma_start(
-                    out=out[b0:b0 + RUNS, n, :, :].rearrange("b (p m) f -> p b (m f)", m=MT),
-                    in_=o_sb[:, bh * RUNS:(bh + 1) * RUNS].rearrange("p b m f -> p b (m f)"),
-                )
+                if not last:
+                    evacuate(i >= CHUNKS - 2 and mt % 2 == 1, o_sb[:, :, mt, :],
+                             acc[:].rearrange("p (b f) -> p b f", f=F), n, mt)
+            if last:
+                for bh in range(BG // RUNS):
+                    for mt in range(MT):
+                        evacuate(mt % 2 == 1, o_sb[:, bh * RUNS:(bh + 1) * RUNS, mt, :],
+                                 accs[mt][:, bh * RUNS * F:(bh + 1) * RUNS * F].rearrange("p (b f) -> p b f", f=F),
+                                 n, mt)
+                    store(i, o_sb, bh)
+            else:
+                for bh in range(BG // RUNS):
+                    store(i, o_sb, bh)
 
         def s_conv(half):
             return half >= 2 and half % 2 == 0
 
+        done_r = set()
+        done_q = set()
+
+        def do_regroup(i):
+            if 0 <= i < CHUNKS and i not in done_r:
+                done_r.add(i)
+                regroup(i, False)
+
+        def do_quant(i):
+            if 0 <= i < CHUNKS and i not in done_q:
+                done_q.add(i)
+                quant(i)
+
         for p in range(-SIG_LEAD, CHUNKS):
-            if 2 <= p + LOAD_LEAD < CHUNKS:
+            if RAW_BUFS <= p + LOAD_LEAD < CHUNKS:
                 load(p + LOAD_LEAD)
             if 0 <= p + SIG_LEAD < PIECES:
                 sig(p + SIG_LEAD)
-            qprev = p - 1 + PROD_LEAD
-            if 0 <= qprev < PIECES and qprev % 2 == 1 and s_conv(qprev // 2):
-                conv(qprev // 2, True)
-            den_half = qprev // 2 if (0 <= qprev < PIECES and qprev % 2 == 1) else None
-            if p >= 0:
-                multiply(p, den_half)
-            elif den_half is not None:
-                for mt in range(MT):
-                    den(den_half, mt)
             q = p + PROD_LEAD
-            qpp = qprev - 1
+            qprev = q - 1
+            qpp = q - 2
+            s_fin = 0 <= qprev < PIECES and qprev % 2 == 1 and s_conv(qprev // 2)
+            if s_fin:
+                conv(qprev // 2, True)
+            if p >= 0:
+                multiply(p)
+            if 0 <= qprev < PIECES and qprev % 4 == 3:
+                den(qprev // 4)
             if 0 <= qpp < PIECES and qpp % 4 == 3:
                 rden_of(qpp // 4)
+            if p == -7:
+                do_regroup(1)
+                do_quant(0)
+            if p == -6:
+                do_regroup(2)
+            if p == -5:
+                do_quant(1)
             if 0 <= q < PIECES:
                 prod(q)
-            if 0 <= p + XQ_LEAD < CHUNKS:
-                quant(p + XQ_LEAD)
+            do_quant(p + XQ_LEAD)
             v_fin = 0 <= q < PIECES and q % 2 == 1 and not s_conv(q // 2)
             if v_fin:
                 conv(q // 2, False)
-            if 0 <= p + XR_LEAD < CHUNKS:
-                regroup(p + XR_LEAD, False)
+            do_regroup(p + XR_LEAD)
             if v_fin:
                 qa(q // 2)
-            if 0 <= qprev < PIECES and qprev % 2 == 1 and s_conv(qprev // 2):
+            if s_fin:
                 qa(qprev // 2)

@@ -120,89 +120,78 @@ def tile_weightedaggregation_t_kernel(tc, x_aug, t, t_left, t_right, kappa, out)
         fact = const.tile([P, 2, W], F32)
         fac = 1.0
         for i in range(W):
-            nc.vector.memset(fact[:, 0, i:i + 1], fac)
-            nc.vector.memset(fact[:, 1, i:i + 1], float(2 * i + 1))
+            nc.vector.memset(fact[:, 0, W - 1 - i:W - i], fac)
+            nc.vector.memset(fact[:, 1, W - 1 - i:W - i], float(2 * i + 1))
             fac = fac * (i + 1)
         coef = const.tile([P, 2, W], F32)
         nc.vector.reciprocal(out=coef[:], in_=fact[:])
-        tp = const.tile([P, N, W], F32)
-        nc.vector.memset(tp[:], 1.0)
-        up = const.tile([P, N, W], F32)
-        nc.vector.memset(up[:], 1.0)
 
         regroup(0, True)
 
         trp = const.tile([P, N, M], BF16)
         tlp = const.tile([P, N, M], BF16)
         for n in range(N):
-            for src, dst in ((trb, trp), (tlb, tlp)):
+            for src, dst, sign in ((trb, trp, 1.0), (tlb, tlp, -1.0)):
                 nc.gpsimd.tensor_scalar(
                     out=dst[:, n, :].rearrange("p (j q) -> p j q", j=MT),
                     in0=src[:, n, :].rearrange("p (q j) -> p j q", j=MT),
-                    scalar1=1.0, scalar2=0.0, op0=ALU.mult, op1=ALU.add,
+                    scalar1=sign, scalar2=0.0, op0=ALU.mult, op1=ALU.add,
                 )
 
-        def powers(pt):
-            nc.vector.tensor_tensor(out=pt[:, :, 2:3], in0=pt[:, :, 1:2], in1=pt[:, :, 1:2], op=ALU.mult)
-            for lo in (2, 4, 8):
-                nc.vector.tensor_tensor(
-                    out=pt[:, :, lo + 1:2 * lo + 1], in0=pt[:, :, 1:lo + 1],
-                    in1=pt[:, :, lo:lo + 1].to_broadcast([P, N, lo]), op=ALU.mult,
+        def series(arg, row, name):
+            states = const.tile([P, N, W], F32, name="states_" + name)
+            for n in range(N):
+                nc.vector.tensor_tensor_scan(
+                    out=states[:, n, :], data0=arg[:, n:n + 1].to_broadcast([P, W]), data1=coef[:, row, :],
+                    initial=0.0, op0=ALU.mult, op1=ALU.add,
                 )
+            return states[:, :, W - 1]
 
-        def series(pt, row, name):
-            powers(pt)
-            terms = const.tile([P, N, W], F32, name="terms_" + name)
-            nc.vector.tensor_tensor(out=terms[:], in0=pt[:], in1=coef[:, row:row + 1, :].to_broadcast([P, N, W]),
-                                    op=ALU.mult)
-            total = const.tile([P, N], F32, name="total_" + name)
-            nc.vector.tensor_reduce(out=total[:], in_=terms[:], axis=AX.X, op=ALU.add)
-            return total
-
-        kap = const.tile([P, N], F32)
-        nc.vector.tensor_copy(out=kap[:], in_=kap_bf[:])
+        a0 = const.tile([P, N], F32)
+        nc.vector.scalar_tensor_tensor(out=a0[:], in0=kap_bf[:], scalar=-1.0, in1=kap_bf[:], op0=ALU.mult, op1=ALU.max)
         tt = const.tile([P, CJ], F32)
         nc.vector.tensor_copy(out=tt[:], in_=tt_bf[:].rearrange("p c j -> p (c j)"))
-        a0 = const.tile([P, N], F32)
-        nc.vector.scalar_tensor_tensor(out=a0[:], in0=kap[:], scalar=-1.0, in1=kap[:], op0=ALU.mult, op1=ALU.max)
         aa = const.tile([P, N], F32)
         nc.vector.tensor_scalar(out=aa[:], in0=a0[:], scalar1=80.0, scalar2=None, op0=ALU.min)
+        ntt = const.tile([P, CJ], F32)
+        nc.vector.tensor_scalar(out=ntt[:], in0=tt[:], scalar1=-1.0, scalar2=None, op0=ALU.mult)
         n_i = const.tile([P, N], I32)
         nc.vector.tensor_scalar(out=n_i[:], in0=aa[:], scalar1=LOG2E, scalar2=None, op0=ALU.mult)
         nfl = const.tile([P, N], F32)
         nc.vector.tensor_copy(out=nfl[:], in_=n_i[:])
-        r1 = const.tile([P, N], F32)
-        nc.vector.scalar_tensor_tensor(out=r1[:], in0=nfl[:], scalar=LN2_HI, in1=aa[:], op0=ALU.mult, op1=ALU.subtract)
-        nc.vector.scalar_tensor_tensor(out=tp[:, :, 1], in0=nfl[:], scalar=LN2_LO, in1=r1[:], op0=ALU.mult, op1=ALU.add)
         e_i = const.tile([P, N], I32)
         nc.vector.tensor_scalar(out=e_i[:], in0=n_i[:], scalar1=-1.0, scalar2=127.0, op0=ALU.mult, op1=ALU.add)
+        r1 = const.tile([P, N], F32)
+        nc.vector.scalar_tensor_tensor(out=r1[:], in0=nfl[:], scalar=LN2_HI, in1=aa[:], op0=ALU.mult, op1=ALU.subtract)
         p_i = const.tile([P, N], I32)
         nc.vector.tensor_single_scalar(out=p_i[:], in_=e_i[:], scalar=23, op=ALU.logical_shift_left)
-        er = series(tp, 0, "exp")
+        rr = const.tile([P, N], F32)
+        nc.vector.scalar_tensor_tensor(out=rr[:], in0=nfl[:], scalar=LN2_LO, in1=r1[:], op0=ALU.mult, op1=ALU.add)
+        er = series(rr, 0, "exp")
         yy = const.tile([P, N], F32)
-        nc.vector.tensor_tensor(out=yy[:], in0=er[:], in1=p_i[:].bitcast(F32), op=ALU.mult)
+        nc.vector.tensor_tensor(out=yy[:], in0=er, in1=p_i[:].bitcast(F32), op=ALU.mult)
         dd = const.tile([P, N], F32)
         nc.vector.tensor_scalar(out=dd[:], in0=yy[:], scalar1=2.0, scalar2=None, op0=ALU.add)
         rd = const.tile([P, N], F32)
         nc.vector.reciprocal(out=rd[:], in_=dd[:])
         ss = const.tile([P, N], F32)
         nc.vector.tensor_tensor(out=ss[:], in0=yy[:], in1=rd[:], op=ALU.mult)
-        nc.vector.tensor_tensor(out=up[:, :, 1], in0=ss[:], in1=ss[:], op=ALU.mult)
-        pl = series(up, 1, "log")
+        uu = const.tile([P, N], F32)
+        nc.vector.tensor_tensor(out=uu[:], in0=ss[:], in1=ss[:], op=ALU.mult)
+        pl = series(uu, 1, "log")
         l1p = const.tile([P, N], F32)
-        nc.vector.scalar_tensor_tensor(out=l1p[:], in0=pl[:], scalar=2.0, in1=ss[:], op0=ALU.mult, op1=ALU.mult)
+        nc.vector.scalar_tensor_tensor(out=l1p[:], in0=pl, scalar=2.0, in1=ss[:], op0=ALU.mult, op1=ALU.mult)
         kk = const.tile([P, N], F32)
-        nc.vector.scalar_tensor_tensor(out=kk[:], in0=kap[:], scalar=0.0, in1=l1p[:], op0=ALU.max, op1=ALU.add)
+        nc.vector.scalar_tensor_tensor(out=kk[:], in0=kap_bf[:], scalar=0.0, in1=l1p[:], op0=ALU.max, op1=ALU.add)
         rk = const.tile([P, N], F32)
         nc.vector.reciprocal(out=rk[:], in_=kk[:])
-        nrk = const.tile([P, N], F32)
-        nc.vector.tensor_scalar(out=nrk[:], in0=rk[:], scalar1=-1.0, scalar2=None, op0=ALU.mult)
 
+        nbt = const.tile([P, N, CJ], F32)
+        nc.vector.tensor_tensor(out=nbt[:], in0=ntt[:].unsqueeze(1).to_broadcast([P, N, CJ]),
+                                in1=rk[:].unsqueeze(2).to_broadcast([P, N, CJ]), op=ALU.mult)
         bt = const.tile([P, N, CJ], F32)
         nc.vector.tensor_tensor(out=bt[:], in0=tt[:].unsqueeze(1).to_broadcast([P, N, CJ]),
                                 in1=rk[:].unsqueeze(2).to_broadcast([P, N, CJ]), op=ALU.mult)
-        nbt = const.tile([P, N, CJ], F32)
-        nc.vector.tensor_scalar(out=nbt[:], in0=bt[:], scalar1=-1.0, scalar2=None, op0=ALU.mult)
 
         rden = const.tile([P, N, MT], F32)
         a_codes = []
@@ -223,7 +212,7 @@ def tile_weightedaggregation_t_kernel(tc, x_aug, t, t_left, t_right, kappa, out)
                 nc.scalar.activation(out=s1[:, e, :], in_=trp[:, n, :], func=ACT.Sigmoid,
                                      bias=nbt[:, n, cj:cj + 1], scale=rk[:, n:n + 1])
                 nc.scalar.activation(out=s2[:, e, :], in_=tlp[:, n, :], func=ACT.Sigmoid,
-                                     bias=bt[:, n, cj:cj + 1], scale=nrk[:, n:n + 1])
+                                     bias=bt[:, n, cj:cj + 1], scale=rk[:, n:n + 1])
             st[("s", q)] = (s1, s2)
 
         def prod(q):
@@ -266,12 +255,17 @@ def tile_weightedaggregation_t_kernel(tc, x_aug, t, t_left, t_right, kappa, out)
                         start=(cj == 0), stop=(cj == CJ - 1),
                     )
 
-        def rden_of(n):
-            dsum = const.tile([P, MT], F32, name="dsum%d" % n)
-            nc.vector.tensor_reduce(out=dsum[:], in_=st[("d", n)][:], axis=AX.X, op=ALU.add)
-            dse = const.tile([P, MT], F32, name="dse%d" % n)
-            nc.vector.tensor_scalar(out=dse[:], in0=dsum[:], scalar1=EPS, scalar2=None, op0=ALU.add)
-            nc.vector.reciprocal(out=rden[:, n, :], in_=dse[:])
+        def rden_step(n, step):
+            if step == 0:
+                dsum = const.tile([P, MT], F32, name="dsum%d" % n)
+                nc.vector.tensor_reduce(out=dsum[:], in_=st[("d", n)][:], axis=AX.X, op=ALU.add)
+                st[("ds", n)] = dsum
+            elif step == 1:
+                dse = const.tile([P, MT], F32, name="dse%d" % n)
+                nc.vector.tensor_scalar(out=dse[:], in0=st[("ds", n)][:], scalar1=EPS, scalar2=None, op0=ALU.add)
+                st[("de", n)] = dse
+            else:
+                nc.vector.reciprocal(out=rden[:, n, :], in_=st[("de", n)][:])
 
         def quant(i):
             xg = xgs[i]
@@ -293,7 +287,7 @@ def tile_weightedaggregation_t_kernel(tc, x_aug, t, t_left, t_right, kappa, out)
         def store(i, o_sb, bh):
             n, g = divmod(i, NG)
             b0 = g * BG + bh * RUNS
-            nc.scalar.dma_start(
+            nc.sync.dma_start(
                 out=out[b0:b0 + RUNS, n, :, :].rearrange("b (p m) f -> p b (m f)", m=MT),
                 in_=o_sb[:, bh * RUNS:(bh + 1) * RUNS].rearrange("p b m f -> p b (m f)"),
             )
@@ -361,8 +355,9 @@ def tile_weightedaggregation_t_kernel(tc, x_aug, t, t_left, t_right, kappa, out)
                 multiply(p)
             if 0 <= qprev < PIECES and qprev % 4 == 3:
                 den(qprev // 4)
-            if 0 <= qpp < PIECES and qpp % 4 == 3:
-                rden_of(qpp // 4)
+            r_due = 0 <= qpp < PIECES and qpp % 4 == 3
+            if r_due:
+                rden_step(qpp // 4, 0)
             if p == -7:
                 do_regroup(1)
                 do_quant(0)
@@ -372,7 +367,11 @@ def tile_weightedaggregation_t_kernel(tc, x_aug, t, t_left, t_right, kappa, out)
                 do_quant(1)
             if 0 <= q < PIECES:
                 prod(q)
+            if r_due:
+                rden_step(qpp // 4, 1)
             do_quant(p + XQ_LEAD)
+            if r_due:
+                rden_step(qpp // 4, 2)
             v_fin = 0 <= q < PIECES and q % 2 == 1 and not s_conv(q // 2)
             if v_fin:
                 conv(q // 2, False)

@@ -31,12 +31,12 @@ LOG2E = 1.4426950408889634
 LN2_HI = 0.693145751953125
 LN2_LO = 1.4286068203094173e-06
 
-LOAD_LEAD = 7
+LOAD_LEAD = 9
 SIG_LEAD = 8
 PROD_LEAD = 7
 XR_LEAD = 4
 XQ_LEAD = 3
-RAW_BUFS = 5
+RAW_BUFS = 7
 RUNS = 4
 
 FLOPS = 2 * B * N * M * L * F
@@ -47,7 +47,7 @@ def tile_weightedaggregation_t_kernel(tc, x_aug, t, t_left, t_right, kappa, out)
     with ExitStack() as ctx:
         const = ctx.enter_context(tc.tile_pool(name="const", bufs=1))
         rawp = ctx.enter_context(tc.tile_pool(name="rawp", bufs=RAW_BUFS))
-        xgp = ctx.enter_context(tc.tile_pool(name="xgp", bufs=3))
+        xgp = ctx.enter_context(tc.tile_pool(name="xgp", bufs=2))
         xcp = ctx.enter_context(tc.tile_pool(name="xcp", bufs=4))
         outp = ctx.enter_context(tc.tile_pool(name="outp", bufs=4))
         sgp = ctx.enter_context(tc.tile_pool(name="sgp", bufs=3))
@@ -311,7 +311,7 @@ def tile_weightedaggregation_t_kernel(tc, x_aug, t, t_left, t_right, kappa, out)
                         start=(c == 0), stop=(c == PASSES - 1),
                     )
                 if not last:
-                    evacuate(i >= CHUNKS - 2 and mt % 2 == 1, o_sb[:, :, mt, :],
+                    evacuate(False, o_sb[:, :, mt, :],
                              acc[:].rearrange("p (b f) -> p b f", f=F), n, mt)
             if last:
                 for bh in range(BG // RUNS):
@@ -325,7 +325,7 @@ def tile_weightedaggregation_t_kernel(tc, x_aug, t, t_left, t_right, kappa, out)
                     store(i, o_sb, bh)
 
         def s_conv(half):
-            return half >= 2 and half % 2 == 0
+            return half in (2, 4)
 
         done_r = set()
         done_q = set()

@@ -30,13 +30,14 @@ W = 17
 LOG2E = 1.4426950408889634
 LN2_HI = 0.693145751953125
 LN2_LO = 1.4286068203094173e-06
+WL = 34
 
-LOAD_LEAD = 9
+LOAD_LEAD = 7
 SIG_LEAD = 8
 PROD_LEAD = 7
 XR_LEAD = 4
 XQ_LEAD = 3
-RAW_BUFS = 7
+RAW_BUFS = 5
 RUNS = 4
 
 FLOPS = 2 * B * N * M * L * F
@@ -47,12 +48,12 @@ def tile_weightedaggregation_t_kernel(tc, x_aug, t, t_left, t_right, kappa, out)
     with ExitStack() as ctx:
         const = ctx.enter_context(tc.tile_pool(name="const", bufs=1))
         rawp = ctx.enter_context(tc.tile_pool(name="rawp", bufs=RAW_BUFS))
-        xgp = ctx.enter_context(tc.tile_pool(name="xgp", bufs=2))
+        xgp = ctx.enter_context(tc.tile_pool(name="xgp", bufs=3))
         xcp = ctx.enter_context(tc.tile_pool(name="xcp", bufs=4))
         outp = ctx.enter_context(tc.tile_pool(name="outp", bufs=4))
-        sgp = ctx.enter_context(tc.tile_pool(name="sgp", bufs=3))
-        a32p = ctx.enter_context(tc.tile_pool(name="a32p", bufs=3))
-        gp = ctx.enter_context(tc.tile_pool(name="gp", bufs=2))
+        sgp = ctx.enter_context(tc.tile_pool(name="sgp", bufs=2))
+        a32p = ctx.enter_context(tc.tile_pool(name="a32p", bufs=2))
+        gp = ctx.enter_context(tc.tile_pool(name="gp", bufs=1))
         accp = ctx.enter_context(tc.psum_pool(name="accp", bufs=6))
         denp = ctx.enter_context(tc.psum_pool(name="denp", bufs=2))
         ctx.enter_context(tc.manual_schedule())
@@ -77,14 +78,12 @@ def tile_weightedaggregation_t_kernel(tc, x_aug, t, t_left, t_right, kappa, out)
             n, g = divmod(i, NG)
             raw = rawp.tile([P, PASSES, BG, PACK * F], BF16, name="raw")
             for c in range(PASSES):
-                for bh in range(BG // RUNS):
-                    b0 = g * BG + bh * RUNS
-                    nc.sync.dma_start(
-                        out=raw[:, c, bh * RUNS:(bh + 1) * RUNS, :],
-                        in_=x_aug[b0:b0 + RUNS, n, c * K_PASS:(c + 1) * K_PASS, :].rearrange(
-                            "b (p j) f -> p b (j f)", j=PACK
-                        ),
-                    )
+                nc.sync.dma_start(
+                    out=raw[:, c],
+                    in_=x_aug[g * BG:(g + 1) * BG, n, c * K_PASS:(c + 1) * K_PASS, :].rearrange(
+                        "b (p j) f -> p b (j f)", j=PACK
+                    ),
+                )
             raws[i] = raw
 
         def regroup(i, on_scalar):
@@ -117,14 +116,20 @@ def tile_weightedaggregation_t_kernel(tc, x_aug, t, t_left, t_right, kappa, out)
         make_identity(nc, ident[:])
         warm = const.tile([P, 2], F32)
         nc.scalar.activation(out=warm[:], in_=ones[:], func=ACT.Sigmoid)
-        fact = const.tile([P, 2, W], F32)
+        fact_e = const.tile([P, W], F32)
         fac = 1.0
         for i in range(W):
-            nc.vector.memset(fact[:, 0, W - 1 - i:W - i], fac)
-            nc.vector.memset(fact[:, 1, W - 1 - i:W - i], float(2 * i + 1))
+            nc.vector.memset(fact_e[:, W - 1 - i:W - i], fac)
             fac = fac * (i + 1)
-        coef = const.tile([P, 2, W], F32)
-        nc.vector.reciprocal(out=coef[:], in_=fact[:])
+        coef_e = const.tile([P, W], F32)
+        nc.vector.reciprocal(out=coef_e[:], in_=fact_e[:])
+        fact_l = const.tile([P, WL], F32)
+        nc.vector.memset(fact_l[:], 1.0)
+        for i in range(1, WL, 2):
+            nc.vector.memset(fact_l[:, WL - 1 - i:WL - i], i / 2.0)
+        coef_l = const.tile([P, WL], F32)
+        nc.vector.reciprocal(out=coef_l[:], in_=fact_l[:])
+        nc.vector.memset(coef_l[:].rearrange("p (a b) -> p a b", b=2)[:, :, 1], 0.0)
 
         regroup(0, True)
 
@@ -138,14 +143,14 @@ def tile_weightedaggregation_t_kernel(tc, x_aug, t, t_left, t_right, kappa, out)
                     scalar1=sign, scalar2=0.0, op0=ALU.mult, op1=ALU.add,
                 )
 
-        def series(arg, row, name):
-            states = const.tile([P, N, W], F32, name="states_" + name)
+        def series(arg, coef, width, name):
+            states = const.tile([P, N, width], F32, name="states_" + name)
             for n in range(N):
                 nc.vector.tensor_tensor_scan(
-                    out=states[:, n, :], data0=arg[:, n:n + 1].to_broadcast([P, W]), data1=coef[:, row, :],
+                    out=states[:, n, :], data0=arg[:, n:n + 1].to_broadcast([P, width]), data1=coef[:],
                     initial=0.0, op0=ALU.mult, op1=ALU.add,
                 )
-            return states[:, :, W - 1]
+            return states[:, :, width - 1]
 
         a0 = const.tile([P, N], F32)
         nc.vector.scalar_tensor_tensor(out=a0[:], in0=kap_bf[:], scalar=-1.0, in1=kap_bf[:], op0=ALU.mult, op1=ALU.max)
@@ -167,7 +172,7 @@ def tile_weightedaggregation_t_kernel(tc, x_aug, t, t_left, t_right, kappa, out)
         nc.vector.tensor_single_scalar(out=p_i[:], in_=e_i[:], scalar=23, op=ALU.logical_shift_left)
         rr = const.tile([P, N], F32)
         nc.vector.scalar_tensor_tensor(out=rr[:], in0=nfl[:], scalar=LN2_LO, in1=r1[:], op0=ALU.mult, op1=ALU.add)
-        er = series(rr, 0, "exp")
+        er = series(rr, coef_e, W, "exp")
         yy = const.tile([P, N], F32)
         nc.vector.tensor_tensor(out=yy[:], in0=er, in1=p_i[:].bitcast(F32), op=ALU.mult)
         dd = const.tile([P, N], F32)
@@ -176,13 +181,9 @@ def tile_weightedaggregation_t_kernel(tc, x_aug, t, t_left, t_right, kappa, out)
         nc.vector.reciprocal(out=rd[:], in_=dd[:])
         ss = const.tile([P, N], F32)
         nc.vector.tensor_tensor(out=ss[:], in0=yy[:], in1=rd[:], op=ALU.mult)
-        uu = const.tile([P, N], F32)
-        nc.vector.tensor_tensor(out=uu[:], in0=ss[:], in1=ss[:], op=ALU.mult)
-        pl = series(uu, 1, "log")
-        l1p = const.tile([P, N], F32)
-        nc.vector.scalar_tensor_tensor(out=l1p[:], in0=pl, scalar=2.0, in1=ss[:], op0=ALU.mult, op1=ALU.mult)
+        l1p = series(ss, coef_l, WL, "log")
         kk = const.tile([P, N], F32)
-        nc.vector.scalar_tensor_tensor(out=kk[:], in0=kap_bf[:], scalar=0.0, in1=l1p[:], op0=ALU.max, op1=ALU.add)
+        nc.vector.scalar_tensor_tensor(out=kk[:], in0=kap_bf[:], scalar=0.0, in1=l1p, op0=ALU.max, op1=ALU.add)
         rk = const.tile([P, N], F32)
         nc.vector.reciprocal(out=rk[:], in_=kk[:])
 
@@ -205,40 +206,47 @@ def tile_weightedaggregation_t_kernel(tc, x_aug, t, t_left, t_right, kappa, out)
         def sig(q):
             n, g = divmod(q, 4)
             c, h = divmod(g, 2)
-            s1 = sgp.tile([P, 2, M], F32, name="s1")
-            s2 = sgp.tile([P, 2, M], F32, name="s2")
-            for e in range(2):
-                cj = c * PACK + 2 * h + e
-                nc.scalar.activation(out=s1[:, e, :], in_=trp[:, n, :], func=ACT.Sigmoid,
-                                     bias=nbt[:, n, cj:cj + 1], scale=rk[:, n:n + 1])
-                nc.scalar.activation(out=s2[:, e, :], in_=tlp[:, n, :], func=ACT.Sigmoid,
-                                     bias=bt[:, n, cj:cj + 1], scale=rk[:, n:n + 1])
-            st[("s", q)] = (s1, s2)
-
-        def prod(q):
-            h = q % 2
             if h == 0:
-                a32 = a32p.tile([P, PACK, M], F32, name="a32")
-                st[("a", q // 2)] = a32
-            a32 = st[("a", q // 2)]
-            s1, s2 = st[("s", q)]
-            nc.vector.tensor_tensor(out=a32[:, 2 * h:2 * h + 2, :], in0=s1[:], in1=s2[:], op=ALU.mult)
+                s1 = sgp.tile([P, PACK, M], F32, name="s1")
+                s2 = sgp.tile([P, PACK, M], F32, name="s2")
+                st[("s", q // 2)] = (s1, s2)
+            s1, s2 = st[("s", q // 2)]
+            for j in (2 * h, 2 * h + 1):
+                cj = c * PACK + j
+                nc.scalar.activation(out=s1[:, j, :], in_=trp[:, n, :], func=ACT.Sigmoid,
+                                     bias=nbt[:, n, cj:cj + 1], scale=rk[:, n:n + 1])
+                nc.scalar.activation(out=s2[:, j, :], in_=tlp[:, n, :], func=ACT.Sigmoid,
+                                     bias=bt[:, n, cj:cj + 1], scale=rk[:, n:n + 1])
 
-        def conv(half, on_scalar):
-            a32 = st[("a", half)]
-            grp = gp.tile([P, M, PACK], BF16, name="grp", align_bytes=64)
-            if on_scalar:
-                nc.scalar.copy(out=grp[:], in_=a32[:].rearrange("p j w -> p w j"))
-            else:
-                nc.vector.tensor_copy(out=grp[:], in_=a32[:].rearrange("p j w -> p w j"))
-            st[("g", half)] = grp
-
-        def qa(half):
+        def prod(half):
             n, c = divmod(half, 2)
+            if c == 0:
+                a32 = a32p.tile([P, CJ, M], F32, name="a32")
+                st[("a", n)] = a32
+            s1, s2 = st[("s", half)]
+            nc.vector.tensor_tensor(out=st[("a", n)][:, c * PACK:(c + 1) * PACK, :], in0=s1[:], in1=s2[:], op=ALU.mult)
+
+        def conv(n, passes, on_scalar):
+            a32 = st[("a", n)]
+            if ("g", n) not in st:
+                grp = gp.tile([P, PASSES, M, PACK], BF16, name="grp", align_bytes=64)
+                st[("g", n)] = grp
+            grp = st[("g", n)]
+            if len(passes) == PASSES:
+                nc.vector.tensor_copy(out=grp[:], in_=a32[:].rearrange("p (c j) w -> p c w j", j=PACK))
+            else:
+                c = passes[0]
+                src = a32[:, c * PACK:(c + 1) * PACK, :].rearrange("p j w -> p w j")
+                if on_scalar:
+                    nc.scalar.copy(out=grp[:, c], in_=src)
+                else:
+                    nc.vector.tensor_copy(out=grp[:, c], in_=src)
+
+        def qa(n):
             nc.vector.quantize_mx(
-                out=a_codes[n][:, c, :].bitcast(FP8X4),
-                scales=a_scales[n][:, c, :],
-                in_=st[("g", half)][:].rearrange("p w j -> p (w j)"),
+                out=a_codes[n][:].rearrange("p c w -> p (c w)").bitcast(FP8X4),
+                scales=a_scales[n][:].rearrange("p c w -> p (c w)"),
+                in_=st[("g", n)][:].rearrange("p c w j -> p (c w j)"),
             )
 
         def den(n):
@@ -246,10 +254,9 @@ def tile_weightedaggregation_t_kernel(tc, x_aug, t, t_left, t_right, kappa, out)
             st[("d", n)] = den_ps
             for mt in range(MT):
                 for cj in range(CJ):
-                    c, j = divmod(cj, PACK)
                     nc.tensor.matmul(
                         out=den_ps[:, mt, :],
-                        lhsT=st[("a", 2 * n + c)][:, j, mt * P:(mt + 1) * P],
+                        lhsT=st[("a", n)][:, cj, mt * P:(mt + 1) * P],
                         rhs=ident[:],
                         is_transpose=True,
                         start=(cj == 0), stop=(cj == CJ - 1),
@@ -284,12 +291,12 @@ def tile_weightedaggregation_t_kernel(tc, x_aug, t, t_left, t_right, kappa, out)
             else:
                 nc.scalar.activation(out=dst, in_=src, func=ACT.Copy, scale=rden[:, n, mt:mt + 1])
 
-        def store(i, o_sb, bh):
+        def store(i, o_sb, lo, count):
             n, g = divmod(i, NG)
-            b0 = g * BG + bh * RUNS
+            b0 = g * BG + lo
             nc.sync.dma_start(
-                out=out[b0:b0 + RUNS, n, :, :].rearrange("b (p m) f -> p b (m f)", m=MT),
-                in_=o_sb[:, bh * RUNS:(bh + 1) * RUNS].rearrange("p b m f -> p b (m f)"),
+                out=out[b0:b0 + count, n, :, :].rearrange("b (p m) f -> p b (m f)", m=MT),
+                in_=o_sb[:, lo:lo + count].rearrange("p b m f -> p b (m f)"),
             )
 
         def multiply(i):
@@ -311,7 +318,7 @@ def tile_weightedaggregation_t_kernel(tc, x_aug, t, t_left, t_right, kappa, out)
                         start=(c == 0), stop=(c == PASSES - 1),
                     )
                 if not last:
-                    evacuate(False, o_sb[:, :, mt, :],
+                    evacuate(i >= CHUNKS - 2 and mt % 2 == 1, o_sb[:, :, mt, :],
                              acc[:].rearrange("p (b f) -> p b f", f=F), n, mt)
             if last:
                 for bh in range(BG // RUNS):
@@ -319,13 +326,12 @@ def tile_weightedaggregation_t_kernel(tc, x_aug, t, t_left, t_right, kappa, out)
                         evacuate(mt % 2 == 1, o_sb[:, bh * RUNS:(bh + 1) * RUNS, mt, :],
                                  accs[mt][:, bh * RUNS * F:(bh + 1) * RUNS * F].rearrange("p (b f) -> p b f", f=F),
                                  n, mt)
-                    store(i, o_sb, bh)
+                    store(i, o_sb, bh * RUNS, RUNS)
             else:
-                for bh in range(BG // RUNS):
-                    store(i, o_sb, bh)
+                store(i, o_sb, 0, BG)
 
-        def s_conv(half):
-            return half in (2, 4)
+        def s_conv(n):
+            return n >= 1
 
         done_r = set()
         done_q = set()
@@ -348,9 +354,8 @@ def tile_weightedaggregation_t_kernel(tc, x_aug, t, t_left, t_right, kappa, out)
             q = p + PROD_LEAD
             qprev = q - 1
             qpp = q - 2
-            s_fin = 0 <= qprev < PIECES and qprev % 2 == 1 and s_conv(qprev // 2)
-            if s_fin:
-                conv(qprev // 2, True)
+            if 0 <= qprev < PIECES and qprev % 4 == 1 and s_conv(qprev // 4):
+                conv(qprev // 4, (0,), True)
             if p >= 0:
                 multiply(p)
             if 0 <= qprev < PIECES and qprev % 4 == 3:
@@ -365,18 +370,16 @@ def tile_weightedaggregation_t_kernel(tc, x_aug, t, t_left, t_right, kappa, out)
                 do_regroup(2)
             if p == -5:
                 do_quant(1)
-            if 0 <= q < PIECES:
-                prod(q)
+            if 0 <= q < PIECES and q % 2 == 1:
+                prod(q // 2)
             if r_due:
                 rden_step(qpp // 4, 1)
             do_quant(p + XQ_LEAD)
             if r_due:
                 rden_step(qpp // 4, 2)
-            v_fin = 0 <= q < PIECES and q % 2 == 1 and not s_conv(q // 2)
+            v_fin = 0 <= q < PIECES and q % 4 == 3
             if v_fin:
-                conv(q // 2, False)
+                conv(q // 4, (1,) if s_conv(q // 4) else (0, 1), False)
             do_regroup(p + XR_LEAD)
             if v_fin:
-                qa(q // 2)
-            if s_fin:
-                qa(qprev // 2)
+                qa(q // 4)

@@ -54,20 +54,19 @@ def tile_weightedaggregation_t_kernel(tc, x_aug, t, t_left, t_right, kappa, out)
         sgp = ctx.enter_context(tc.tile_pool(name="sgp", bufs=2))
         a32p = ctx.enter_context(tc.tile_pool(name="a32p", bufs=2))
         gp = ctx.enter_context(tc.tile_pool(name="gp", bufs=1))
-        accp = ctx.enter_context(tc.psum_pool(name="accp", bufs=6))
-        denp = ctx.enter_context(tc.psum_pool(name="denp", bufs=2))
+        accp = ctx.enter_context(tc.psum_pool(name="accp", bufs=5))
+        denp = ctx.enter_context(tc.psum_pool(name="denp", bufs=1))
+        edgep = ctx.enter_context(tc.psum_pool(name="edgep", bufs=1))
         ctx.enter_context(tc.manual_schedule())
 
         kap_bf = const.tile([P, N], BF16)
         nc.sync.dma_start(out=kap_bf[:], in_=kappa.rearrange("n o -> (n o)").partition_broadcast(P))
         tt_bf = const.tile([P, PASSES, PACK], BF16)
         nc.sync.dma_start(out=tt_bf[:], in_=t.rearrange("(c p j) o -> p c (j o)", c=PASSES, j=PACK))
-        trb = const.tile([P, N, M], BF16)
-        nc.scalar.dma_start(out=trb[:].rearrange("p n m -> p (n m)"),
-                            in_=t_right.rearrange("n m -> (n m)").partition_broadcast(P))
-        tlb = const.tile([P, N, M], BF16)
-        nc.scalar.dma_start(out=tlb[:].rearrange("p n m -> p (n m)"),
-                            in_=t_left.rearrange("n m -> (n m)").partition_broadcast(P))
+        edges = const.tile([P, M], BF16)
+        nc.vector.memset(edges[:], 0.0)
+        nc.scalar.dma_start(out=edges[0:N, :], in_=t_right)
+        nc.scalar.dma_start(out=edges[N:2 * N, :], in_=t_left)
 
         raws = {}
         xgs = {}
@@ -114,6 +113,8 @@ def tile_weightedaggregation_t_kernel(tc, x_aug, t, t_left, t_right, kappa, out)
         nc.vector.memset(ones[:], 1.0)
         ident = const.tile([P, P], F32)
         make_identity(nc, ident[:])
+        ident_bf = const.tile([P, P], BF16)
+        make_identity(nc, ident_bf[:])
         warm = const.tile([P, 2], F32)
         nc.scalar.activation(out=warm[:], in_=ones[:], func=ACT.Sigmoid)
         fact_e = const.tile([P, W], F32)
@@ -133,15 +134,18 @@ def tile_weightedaggregation_t_kernel(tc, x_aug, t, t_left, t_right, kappa, out)
 
         regroup(0, True)
 
-        trp = const.tile([P, N, M], BF16)
-        tlp = const.tile([P, N, M], BF16)
-        for n in range(N):
-            for src, dst, sign in ((trb, trp, 1.0), (tlb, tlp, -1.0)):
-                nc.gpsimd.tensor_scalar(
-                    out=dst[:, n, :].rearrange("p (j q) -> p j q", j=MT),
-                    in0=src[:, n, :].rearrange("p (q j) -> p j q", j=MT),
-                    scalar1=sign, scalar2=0.0, op0=ALU.mult, op1=ALU.add,
+        def spread(n):
+            for key, row in (("tr", n), ("tl", N + n)):
+                bank = edgep.tile([P, M], F32, name="e" + key)
+                nc.tensor.matmul(
+                    out=bank[:].rearrange("p (j q) -> p j q", j=MT),
+                    lhsT=ident_bf[:, row:row + 1].to_broadcast([P, P]),
+                    rhs=edges[:].rearrange("p (q j) -> p j q", j=MT),
+                    start=True, stop=True,
                 )
+                st[(key, n)] = bank
+
+        spread(0)
 
         def series(arg, coef, width, name):
             states = const.tile([P, N, width], F32, name="states_" + name)
@@ -186,10 +190,12 @@ def tile_weightedaggregation_t_kernel(tc, x_aug, t, t_left, t_right, kappa, out)
         nc.vector.scalar_tensor_tensor(out=kk[:], in0=kap_bf[:], scalar=0.0, in1=l1p, op0=ALU.max, op1=ALU.add)
         rk = const.tile([P, N], F32)
         nc.vector.reciprocal(out=rk[:], in_=kk[:])
+        nrk = const.tile([P, N], F32)
 
         nbt = const.tile([P, N, CJ], F32)
         nc.vector.tensor_tensor(out=nbt[:], in0=ntt[:].unsqueeze(1).to_broadcast([P, N, CJ]),
                                 in1=rk[:].unsqueeze(2).to_broadcast([P, N, CJ]), op=ALU.mult)
+        nc.vector.tensor_scalar(out=nrk[:], in0=rk[:], scalar1=-1.0, scalar2=None, op0=ALU.mult)
         bt = const.tile([P, N, CJ], F32)
         nc.vector.tensor_tensor(out=bt[:], in0=tt[:].unsqueeze(1).to_broadcast([P, N, CJ]),
                                 in1=rk[:].unsqueeze(2).to_broadcast([P, N, CJ]), op=ALU.mult)
@@ -213,10 +219,12 @@ def tile_weightedaggregation_t_kernel(tc, x_aug, t, t_left, t_right, kappa, out)
             s1, s2 = st[("s", q // 2)]
             for j in (2 * h, 2 * h + 1):
                 cj = c * PACK + j
-                nc.scalar.activation(out=s1[:, j, :], in_=trp[:, n, :], func=ACT.Sigmoid,
+                nc.scalar.activation(out=s1[:, j, :], in_=st[("tr", n)][:], func=ACT.Sigmoid,
                                      bias=nbt[:, n, cj:cj + 1], scale=rk[:, n:n + 1])
-                nc.scalar.activation(out=s2[:, j, :], in_=tlp[:, n, :], func=ACT.Sigmoid,
-                                     bias=bt[:, n, cj:cj + 1], scale=rk[:, n:n + 1])
+            for j in (2 * h, 2 * h + 1):
+                cj = c * PACK + j
+                nc.scalar.activation(out=s2[:, j, :], in_=st[("tl", n)][:], func=ACT.Sigmoid,
+                                     bias=bt[:, n, cj:cj + 1], scale=nrk[:, n:n + 1])
 
         def prod(half):
             n, c = divmod(half, 2)
@@ -358,6 +366,8 @@ def tile_weightedaggregation_t_kernel(tc, x_aug, t, t_left, t_right, kappa, out)
                 conv(qprev // 4, (0,), True)
             if p >= 0:
                 multiply(p)
+            if 0 <= p + SIG_LEAD < PIECES - 4 and (p + SIG_LEAD) % 4 == 3:
+                spread((p + SIG_LEAD) // 4 + 1)
             if 0 <= qprev < PIECES and qprev % 4 == 3:
                 den(qprev // 4)
             r_due = 0 <= qpp < PIECES and qpp % 4 == 3

@@ -302,7 +302,7 @@ def tile_weightedaggregation_t_kernel(tc, x_aug, t, t_left, t_right, kappa, out)
         def store(i, o_sb, lo, count):
             n, g = divmod(i, NG)
             b0 = g * BG + lo
-            nc.sync.dma_start(
+            nc.scalar.dma_start(
                 out=out[b0:b0 + count, n, :, :].rearrange("b (p m) f -> p b (m f)", m=MT),
                 in_=o_sb[:, lo:lo + count].rearrange("p b m f -> p b (m f)"),
             )

@@ -35,6 +35,7 @@ WL = 34
 LOAD_LEAD = 7
 SIG_LEAD = 8
 PROD_LEAD = 7
+TURN_LEAD = 6
 XR_LEAD = 4
 XQ_LEAD = 3
 RAW_BUFS = 5
@@ -52,21 +53,21 @@ def tile_weightedaggregation_t_kernel(tc, x_aug, t, t_left, t_right, kappa, out)
         xcp = ctx.enter_context(tc.tile_pool(name="xcp", bufs=4))
         outp = ctx.enter_context(tc.tile_pool(name="outp", bufs=4))
         sgp = ctx.enter_context(tc.tile_pool(name="sgp", bufs=2))
-        a32p = ctx.enter_context(tc.tile_pool(name="a32p", bufs=2))
-        gp = ctx.enter_context(tc.tile_pool(name="gp", bufs=1))
-        accp = ctx.enter_context(tc.psum_pool(name="accp", bufs=5))
-        denp = ctx.enter_context(tc.psum_pool(name="denp", bufs=1))
-        edgep = ctx.enter_context(tc.psum_pool(name="edgep", bufs=1))
+        atp = ctx.enter_context(tc.tile_pool(name="atp", bufs=2))
+        gp = ctx.enter_context(tc.tile_pool(name="gp", bufs=2))
+        accp = ctx.enter_context(tc.psum_pool(name="accp", bufs=6))
+        turnp = ctx.enter_context(tc.psum_pool(name="turnp", bufs=2))
         ctx.enter_context(tc.manual_schedule())
 
         kap_bf = const.tile([P, N], BF16)
         nc.sync.dma_start(out=kap_bf[:], in_=kappa.rearrange("n o -> (n o)").partition_broadcast(P))
-        tt_bf = const.tile([P, PASSES, PACK], BF16)
-        nc.sync.dma_start(out=tt_bf[:], in_=t.rearrange("(c p j) o -> p c (j o)", c=PASSES, j=PACK))
-        edges = const.tile([P, M], BF16)
-        nc.vector.memset(edges[:], 0.0)
-        nc.scalar.dma_start(out=edges[0:N, :], in_=t_right)
-        nc.scalar.dma_start(out=edges[N:2 * N, :], in_=t_left)
+        trow = const.tile([P, L], BF16)
+        nc.vector.memset(trow[:], 0.0)
+        nc.scalar.dma_start(out=trow[0:1, :], in_=t.rearrange("l o -> o l"))
+        trq = const.tile([P, N, MT], BF16)
+        nc.scalar.dma_start(out=trq[:], in_=t_right.rearrange("n (q j) -> q n j", j=MT))
+        tlq = const.tile([P, N, MT], BF16)
+        nc.scalar.dma_start(out=tlq[:], in_=t_left.rearrange("n (q j) -> q n j", j=MT))
 
         raws = {}
         xgs = {}
@@ -132,20 +133,18 @@ def tile_weightedaggregation_t_kernel(tc, x_aug, t, t_left, t_right, kappa, out)
         nc.vector.reciprocal(out=coef_l[:], in_=fact_l[:])
         nc.vector.memset(coef_l[:].rearrange("p (a b) -> p a b", b=2)[:, :, 1], 0.0)
 
+        t_all = const.tile([P, L], BF16)
+        for c in range(PASSES):
+            bank = turnp.tile([P, K_PASS], F32, name="turn")
+            nc.tensor.matmul(
+                out=bank[:].rearrange("q (u p e) -> q u p e", u=2, e=2),
+                lhsT=ident_bf[:, 0:1].to_broadcast([P, P]),
+                rhs=trow[:, c * K_PASS:(c + 1) * K_PASS].rearrange("r (p u e) -> r u p e", u=2, e=2),
+                start=True, stop=True,
+            )
+            nc.scalar.copy(out=t_all[:, c * K_PASS:(c + 1) * K_PASS], in_=bank[:])
+
         regroup(0, True)
-
-        def spread(n):
-            for key, row in (("tr", n), ("tl", N + n)):
-                bank = edgep.tile([P, M], F32, name="e" + key)
-                nc.tensor.matmul(
-                    out=bank[:].rearrange("p (j q) -> p j q", j=MT),
-                    lhsT=ident_bf[:, row:row + 1].to_broadcast([P, P]),
-                    rhs=edges[:].rearrange("p (q j) -> p j q", j=MT),
-                    start=True, stop=True,
-                )
-                st[(key, n)] = bank
-
-        spread(0)
 
         def series(arg, coef, width, name):
             states = const.tile([P, N, width], F32, name="states_" + name)
@@ -158,12 +157,8 @@ def tile_weightedaggregation_t_kernel(tc, x_aug, t, t_left, t_right, kappa, out)
 
         a0 = const.tile([P, N], F32)
         nc.vector.scalar_tensor_tensor(out=a0[:], in0=kap_bf[:], scalar=-1.0, in1=kap_bf[:], op0=ALU.mult, op1=ALU.max)
-        tt = const.tile([P, CJ], F32)
-        nc.vector.tensor_copy(out=tt[:], in_=tt_bf[:].rearrange("p c j -> p (c j)"))
         aa = const.tile([P, N], F32)
         nc.vector.tensor_scalar(out=aa[:], in0=a0[:], scalar1=80.0, scalar2=None, op0=ALU.min)
-        ntt = const.tile([P, CJ], F32)
-        nc.vector.tensor_scalar(out=ntt[:], in0=tt[:], scalar1=-1.0, scalar2=None, op0=ALU.mult)
         n_i = const.tile([P, N], I32)
         nc.vector.tensor_scalar(out=n_i[:], in0=aa[:], scalar1=LOG2E, scalar2=None, op0=ALU.mult)
         nfl = const.tile([P, N], F32)
@@ -191,15 +186,14 @@ def tile_weightedaggregation_t_kernel(tc, x_aug, t, t_left, t_right, kappa, out)
         rk = const.tile([P, N], F32)
         nc.vector.reciprocal(out=rk[:], in_=kk[:])
         nrk = const.tile([P, N], F32)
-
-        nbt = const.tile([P, N, CJ], F32)
-        nc.vector.tensor_tensor(out=nbt[:], in0=ntt[:].unsqueeze(1).to_broadcast([P, N, CJ]),
-                                in1=rk[:].unsqueeze(2).to_broadcast([P, N, CJ]), op=ALU.mult)
         nc.vector.tensor_scalar(out=nrk[:], in0=rk[:], scalar1=-1.0, scalar2=None, op0=ALU.mult)
-        bt = const.tile([P, N, CJ], F32)
-        nc.vector.tensor_tensor(out=bt[:], in0=tt[:].unsqueeze(1).to_broadcast([P, N, CJ]),
-                                in1=rk[:].unsqueeze(2).to_broadcast([P, N, CJ]), op=ALU.mult)
+        b_r = const.tile([P, N, MT], F32)
+        nc.vector.tensor_tensor(out=b_r[:], in0=trq[:], in1=rk[:].unsqueeze(2).to_broadcast([P, N, MT]), op=ALU.mult)
+        b_l = const.tile([P, N, MT], F32)
+        nc.vector.tensor_tensor(out=b_l[:], in0=tlq[:], in1=nrk[:].unsqueeze(2).to_broadcast([P, N, MT]), op=ALU.mult)
 
+        dsum = const.tile([P, N, MT], F32)
+        dse = const.tile([P, N, MT], F32)
         rden = const.tile([P, N, MT], F32)
         a_codes = []
         a_scales = []
@@ -210,45 +204,39 @@ def tile_weightedaggregation_t_kernel(tc, x_aug, t, t_left, t_right, kappa, out)
             a_scales.append(asc)
 
         def sig(q):
-            n, g = divmod(q, 4)
-            c, h = divmod(g, 2)
-            if h == 0:
-                s1 = sgp.tile([P, PACK, M], F32, name="s1")
-                s2 = sgp.tile([P, PACK, M], F32, name="s2")
-                st[("s", q // 2)] = (s1, s2)
-            s1, s2 = st[("s", q // 2)]
-            for j in (2 * h, 2 * h + 1):
-                cj = c * PACK + j
-                nc.scalar.activation(out=s1[:, j, :], in_=st[("tr", n)][:], func=ACT.Sigmoid,
-                                     bias=nbt[:, n, cj:cj + 1], scale=rk[:, n:n + 1])
-            for j in (2 * h, 2 * h + 1):
-                cj = c * PACK + j
-                nc.scalar.activation(out=s2[:, j, :], in_=st[("tl", n)][:], func=ACT.Sigmoid,
-                                     bias=bt[:, n, cj:cj + 1], scale=nrk[:, n:n + 1])
+            n, mt = divmod(q, MT)
+            s1 = sgp.tile([P, L], F32, name="s1")
+            s2 = sgp.tile([P, L], F32, name="s2")
+            st[("s", q)] = (s1, s2)
+            nc.scalar.activation(out=s1[:], in_=t_all[:], func=ACT.Sigmoid,
+                                 bias=b_r[:, n, mt:mt + 1], scale=nrk[:, n:n + 1])
+            nc.scalar.activation(out=s2[:], in_=t_all[:], func=ACT.Sigmoid,
+                                 bias=b_l[:, n, mt:mt + 1], scale=rk[:, n:n + 1])
 
-        def prod(half):
-            n, c = divmod(half, 2)
-            if c == 0:
-                a32 = a32p.tile([P, CJ, M], F32, name="a32")
-                st[("a", n)] = a32
-            s1, s2 = st[("s", half)]
-            nc.vector.tensor_tensor(out=st[("a", n)][:, c * PACK:(c + 1) * PACK, :], in0=s1[:], in1=s2[:], op=ALU.mult)
+        def prod(q):
+            n, mt = divmod(q, MT)
+            s1, s2 = st[("s", q)]
+            a_t = atp.tile([P, L], BF16, name="a_t")
+            st[("a", q)] = a_t
+            nc.vector.scalar_tensor_tensor(out=a_t[:], in0=s1[:], scalar=1.0, in1=s2[:], op0=ALU.mult, op1=ALU.mult,
+                                           accum_out=dsum[:, n, mt:mt + 1])
 
-        def conv(n, passes, on_scalar):
-            a32 = st[("a", n)]
-            if ("g", n) not in st:
+        def turn(q):
+            words = st[("a", q)][:].bitcast(F32)
+            bank = turnp.tile([P, PACK, P], F32, name="turn")
+            st[("t", q)] = bank
+            for cu in range(PACK):
+                nc.tensor.transpose(bank[:, cu, :], words[:, cu * P:(cu + 1) * P], ident[:])
+
+        def take(q):
+            n, mt = divmod(q, MT)
+            if mt == 0:
                 grp = gp.tile([P, PASSES, M, PACK], BF16, name="grp", align_bytes=64)
                 st[("g", n)] = grp
-            grp = st[("g", n)]
-            if len(passes) == PASSES:
-                nc.vector.tensor_copy(out=grp[:], in_=a32[:].rearrange("p (c j) w -> p c w j", j=PACK))
-            else:
-                c = passes[0]
-                src = a32[:, c * PACK:(c + 1) * PACK, :].rearrange("p j w -> p w j")
-                if on_scalar:
-                    nc.scalar.copy(out=grp[:, c], in_=src)
-                else:
-                    nc.vector.tensor_copy(out=grp[:, c], in_=src)
+            g_words = st[("g", n)][:].rearrange("p c w j -> p (c w j)").bitcast(F32).rearrange(
+                "p (c w u) -> p c w u", c=PASSES, u=2)
+            nc.scalar.copy(out=g_words[:, :, mt * P:(mt + 1) * P, :],
+                           in_=st[("t", q)][:].rearrange("p (c u) w -> p c w u", u=2))
 
         def qa(n):
             nc.vector.quantize_mx(
@@ -257,30 +245,11 @@ def tile_weightedaggregation_t_kernel(tc, x_aug, t, t_left, t_right, kappa, out)
                 in_=st[("g", n)][:].rearrange("p c w j -> p (c w j)"),
             )
 
-        def den(n):
-            den_ps = denp.tile([P, MT, P], F32, name="den_ps")
-            st[("d", n)] = den_ps
-            for mt in range(MT):
-                for cj in range(CJ):
-                    nc.tensor.matmul(
-                        out=den_ps[:, mt, :],
-                        lhsT=st[("a", n)][:, cj, mt * P:(mt + 1) * P],
-                        rhs=ident[:],
-                        is_transpose=True,
-                        start=(cj == 0), stop=(cj == CJ - 1),
-                    )
-
         def rden_step(n, step):
             if step == 0:
-                dsum = const.tile([P, MT], F32, name="dsum%d" % n)
-                nc.vector.tensor_reduce(out=dsum[:], in_=st[("d", n)][:], axis=AX.X, op=ALU.add)
-                st[("ds", n)] = dsum
-            elif step == 1:
-                dse = const.tile([P, MT], F32, name="dse%d" % n)
-                nc.vector.tensor_scalar(out=dse[:], in0=st[("ds", n)][:], scalar1=EPS, scalar2=None, op0=ALU.add)
-                st[("de", n)] = dse
+                nc.vector.tensor_scalar(out=dse[:, n, :], in0=dsum[:, n, :], scalar1=EPS, scalar2=None, op0=ALU.add)
             else:
-                nc.vector.reciprocal(out=rden[:, n, :], in_=st[("de", n)][:])
+                nc.vector.reciprocal(out=rden[:, n, :], in_=dse[:, n, :])
 
         def quant(i):
             xg = xgs[i]
@@ -338,9 +307,6 @@ def tile_weightedaggregation_t_kernel(tc, x_aug, t, t_left, t_right, kappa, out)
             else:
                 store(i, o_sb, 0, BG)
 
-        def s_conv(n):
-            return n >= 1
-
         done_r = set()
         done_q = set()
 
@@ -357,22 +323,19 @@ def tile_weightedaggregation_t_kernel(tc, x_aug, t, t_left, t_right, kappa, out)
         for p in range(-SIG_LEAD, CHUNKS):
             if RAW_BUFS <= p + LOAD_LEAD < CHUNKS:
                 load(p + LOAD_LEAD)
+            q = p + PROD_LEAD
+            qt = p + TURN_LEAD
+            if 0 <= qt < PIECES:
+                turn(qt)
             if 0 <= p + SIG_LEAD < PIECES:
                 sig(p + SIG_LEAD)
-            q = p + PROD_LEAD
-            qprev = q - 1
-            qpp = q - 2
-            if 0 <= qprev < PIECES and qprev % 4 == 1 and s_conv(qprev // 4):
-                conv(qprev // 4, (0,), True)
+            if 0 <= qt < PIECES:
+                take(qt)
             if p >= 0:
                 multiply(p)
-            if 0 <= p + SIG_LEAD < PIECES - 4 and (p + SIG_LEAD) % 4 == 3:
-                spread((p + SIG_LEAD) // 4 + 1)
-            if 0 <= qprev < PIECES and qprev % 4 == 3:
-                den(qprev // 4)
-            r_due = 0 <= qpp < PIECES and qpp % 4 == 3
+            r_due = 0 <= qt < PIECES and qt % MT == MT - 1
             if r_due:
-                rden_step(qpp // 4, 0)
+                rden_step(qt // MT, 0)
             if p == -7:
                 do_regroup(1)
                 do_quant(0)
@@ -380,16 +343,11 @@ def tile_weightedaggregation_t_kernel(tc, x_aug, t, t_left, t_right, kappa, out)
                 do_regroup(2)
             if p == -5:
                 do_quant(1)
-            if 0 <= q < PIECES and q % 2 == 1:
-                prod(q // 2)
+            if 0 <= q < PIECES:
+                prod(q)
             if r_due:
-                rden_step(qpp // 4, 1)
+                rden_step(qt // MT, 1)
             do_quant(p + XQ_LEAD)
-            if r_due:
-                rden_step(qpp // 4, 2)
-            v_fin = 0 <= q < PIECES and q % 4 == 3
-            if v_fin:
-                conv(q // 4, (1,) if s_conv(q // 4) else (0, 1), False)
             do_regroup(p + XR_LEAD)
-            if v_fin:
-                qa(q // 4)
+            if r_due:
+                qa(qt // MT)

@@ -63,11 +63,11 @@ def tile_weightedaggregation_t_kernel(tc, x_aug, t, t_left, t_right, kappa, out)
         nc.sync.dma_start(out=kap_bf[:], in_=kappa.rearrange("n o -> (n o)").partition_broadcast(P))
         trow = const.tile([P, L], BF16)
         nc.vector.memset(trow[:], 0.0)
-        nc.scalar.dma_start(out=trow[0:1, :], in_=t.rearrange("l o -> o l"))
+        nc.sync.dma_start(out=trow[0:1, :], in_=t.rearrange("l o -> o l"))
         trq = const.tile([P, N, MT], BF16)
-        nc.scalar.dma_start(out=trq[:], in_=t_right.rearrange("n (q j) -> q n j", j=MT))
+        nc.sync.dma_start(out=trq[:], in_=t_right.rearrange("n (q j) -> q n j", j=MT))
         tlq = const.tile([P, N, MT], BF16)
-        nc.scalar.dma_start(out=tlq[:], in_=t_left.rearrange("n (q j) -> q n j", j=MT))
+        nc.sync.dma_start(out=tlq[:], in_=t_left.rearrange("n (q j) -> q n j", j=MT))
 
         raws = {}
         xgs = {}
@@ -94,11 +94,15 @@ def tile_weightedaggregation_t_kernel(tc, x_aug, t, t_left, t_right, kappa, out)
             xg = xgs[i]
             if i in S_REGROUP:
                 if on_scalar:
-                    for c in range(PASSES):
-                        nc.scalar.copy(
-                            out=xg[:, c].rearrange("p (b f) j -> p b f j", b=BG),
-                            in_=raw[:, c].rearrange("p b (j f) -> p b f j", j=PACK),
-                        )
+                    nc.scalar.copy(
+                        out=xg[:, 0].rearrange("p (b f) j -> p b f j", b=BG),
+                        in_=raw[:, 0].rearrange("p b (j f) -> p b f j", j=PACK),
+                    )
+                else:
+                    nc.vector.tensor_copy(
+                        out=xg[:, 1].rearrange("p (b g i) j -> p b g j i", b=BG, i=4),
+                        in_=raw[:, 1].rearrange("p b (j g i) -> p b g j i", j=PACK, i=4),
+                    )
             elif not on_scalar:
                 nc.vector.tensor_copy(
                     out=xg[:].rearrange("p c (b g i) j -> p (c b) g j i", b=BG, i=4),
@@ -337,6 +341,7 @@ def tile_weightedaggregation_t_kernel(tc, x_aug, t, t_left, t_right, kappa, out)
             if r_due:
                 rden_step(qt // MT, 0)
             if p == -7:
+                do_regroup(0)
                 do_regroup(1)
                 do_quant(0)
             if p == -6:

@@ -32,13 +32,13 @@ LN2_HI = 0.693145751953125
 LN2_LO = 1.4286068203094173e-06
 WL = 34
 
-LOAD_LEAD = 7
+LOAD_LEAD = 9
 SIG_LEAD = 8
 PROD_LEAD = 7
 TURN_LEAD = 6
 XR_LEAD = 4
 XQ_LEAD = 3
-RAW_BUFS = 5
+RAW_BUFS = 7
 RUNS = 4
 
 FLOPS = 2 * B * N * M * L * F
@@ -49,11 +49,11 @@ def tile_weightedaggregation_t_kernel(tc, x_aug, t, t_left, t_right, kappa, out)
     with ExitStack() as ctx:
         const = ctx.enter_context(tc.tile_pool(name="const", bufs=1))
         rawp = ctx.enter_context(tc.tile_pool(name="rawp", bufs=RAW_BUFS))
-        xgp = ctx.enter_context(tc.tile_pool(name="xgp", bufs=3))
-        xcp = ctx.enter_context(tc.tile_pool(name="xcp", bufs=4))
-        outp = ctx.enter_context(tc.tile_pool(name="outp", bufs=4))
-        sgp = ctx.enter_context(tc.tile_pool(name="sgp", bufs=2))
-        atp = ctx.enter_context(tc.tile_pool(name="atp", bufs=2))
+        xgp = ctx.enter_context(tc.tile_pool(name="xgp", bufs=4))
+        xcp = ctx.enter_context(tc.tile_pool(name="xcp", bufs=5))
+        outp = ctx.enter_context(tc.tile_pool(name="outp", bufs=5))
+        sgp = ctx.enter_context(tc.tile_pool(name="sgp", bufs=3))
+        atp = ctx.enter_context(tc.tile_pool(name="atp", bufs=3))
         gp = ctx.enter_context(tc.tile_pool(name="gp", bufs=2))
         accp = ctx.enter_context(tc.psum_pool(name="accp", bufs=6))
         turnp = ctx.enter_context(tc.psum_pool(name="turnp", bufs=2))

@@ -100,13 +100,13 @@ def tile_weightedaggregation_t_kernel(tc, x_aug, t, t_left, t_right, kappa, out)
                     )
                 else:
                     nc.vector.tensor_copy(
-                        out=xg[:, 1].rearrange("p (b g i) j -> p b g j i", b=BG, i=4),
-                        in_=raw[:, 1].rearrange("p b (j g i) -> p b g j i", j=PACK, i=4),
+                        out=xg[:, 1].rearrange("p (b g i) j -> p b g j i", b=BG, i=8),
+                        in_=raw[:, 1].rearrange("p b (j g i) -> p b g j i", j=PACK, i=8),
                     )
             elif not on_scalar:
                 nc.vector.tensor_copy(
-                    out=xg[:].rearrange("p c (b g i) j -> p (c b) g j i", b=BG, i=4),
-                    in_=raw[:].rearrange("p c b (j g i) -> p (c b) g j i", j=PACK, i=4),
+                    out=xg[:].rearrange("p c (b g i) j -> p (c b) g j i", b=BG, i=8),
+                    in_=raw[:].rearrange("p c b (j g i) -> p (c b) g j i", j=PACK, i=8),
                 )
 
         S_REGROUP = (0,)
@@ -299,7 +299,7 @@ def tile_weightedaggregation_t_kernel(tc, x_aug, t, t_left, t_right, kappa, out)
                         start=(c == 0), stop=(c == PASSES - 1),
                     )
                 if not last:
-                    evacuate(i >= CHUNKS - 2 and mt % 2 == 1, o_sb[:, :, mt, :],
+                    evacuate(False, o_sb[:, :, mt, :],
                              acc[:].rearrange("p (b f) -> p b f", f=F), n, mt)
             if last:
                 for bh in range(BG // RUNS):

@@ -26,11 +26,10 @@ NG = B // BG
 COLS = BG * F
 CHUNKS = N * NG
 PIECES = N * 4
-W = 17
+W = 26
 LOG2E = 1.4426950408889634
 LN2_HI = 0.693145751953125
 LN2_LO = 1.4286068203094173e-06
-WL = 34
 
 LOAD_LEAD = 9
 SIG_LEAD = 8
@@ -116,26 +115,29 @@ def tile_weightedaggregation_t_kernel(tc, x_aug, t, t_left, t_right, kappa, out)
 
         ones = const.tile([P, 2], F32)
         nc.vector.memset(ones[:], 1.0)
+        count = const.tile([P, N, W], F32)
+        nc.gpsimd.iota(count[:].rearrange("p n w -> p (n w)"), pattern=[[0, N], [-1, W]], base=W, channel_multiplier=0,
+                       allow_small_or_imprecise_dtypes=True)
         ident = const.tile([P, P], F32)
         make_identity(nc, ident[:])
         ident_bf = const.tile([P, P], BF16)
         make_identity(nc, ident_bf[:])
         warm = const.tile([P, 2], F32)
         nc.scalar.activation(out=warm[:], in_=ones[:], func=ACT.Sigmoid)
-        fact_e = const.tile([P, W], F32)
-        fac = 1.0
-        for i in range(W):
-            nc.vector.memset(fact_e[:, W - 1 - i:W - i], fac)
-            fac = fac * (i + 1)
-        coef_e = const.tile([P, W], F32)
-        nc.vector.reciprocal(out=coef_e[:], in_=fact_e[:])
-        fact_l = const.tile([P, WL], F32)
-        nc.vector.memset(fact_l[:], 1.0)
-        for i in range(1, WL, 2):
-            nc.vector.memset(fact_l[:, WL - 1 - i:WL - i], i / 2.0)
-        coef_l = const.tile([P, WL], F32)
-        nc.vector.reciprocal(out=coef_l[:], in_=fact_l[:])
-        nc.vector.memset(coef_l[:].rearrange("p (a b) -> p a b", b=2)[:, :, 1], 0.0)
+        step_e = const.tile([P, N, W], F32)
+        nc.vector.reciprocal(out=step_e[:], in_=count[:])
+        nc.vector.memset(step_e[:, :, 0:1], 0.0)
+        unit = const.tile([P, N, W], F32)
+        nc.vector.memset(unit[:], 1.0)
+        half = const.tile([P, N, W], F32)
+        nc.vector.tensor_scalar(out=half[:], in0=count[:], scalar1=-1.0, scalar2=0.5, op0=ALU.add, op1=ALU.mult)
+        coef_l = const.tile([P, N, W], F32)
+        nc.vector.memset(coef_l[:], 0.0)
+        nc.vector.reciprocal(out=coef_l[:].rearrange("p n (a b) -> p n a b", b=2)[:, :, :, 0],
+                             in_=half[:].rearrange("p n (a b) -> p n a b", b=2)[:, :, :, 0])
+        first = const.tile([P, N, W], F32)
+        nc.vector.memset(first[:], 1.0)
+        nc.vector.memset(first[:, :, 0:1], 0.0)
 
         t_all = const.tile([P, L], BF16)
         for c in range(PASSES):
@@ -150,32 +152,36 @@ def tile_weightedaggregation_t_kernel(tc, x_aug, t, t_left, t_right, kappa, out)
 
         regroup(0, True)
 
-        def series(arg, coef, width, name):
-            states = const.tile([P, N, width], F32, name="states_" + name)
-            for n in range(N):
-                nc.vector.tensor_tensor_scan(
-                    out=states[:, n, :], data0=arg[:, n:n + 1].to_broadcast([P, width]), data1=coef[:],
-                    initial=0.0, op0=ALU.mult, op1=ALU.add,
-                )
-            return states[:, :, width - 1]
+        def series(arg, factor, addend, name):
+            steps = const.tile([P, N, W], F32, name="steps_" + name)
+            nc.vector.tensor_tensor(out=steps[:], in0=arg[:].unsqueeze(2).to_broadcast([P, N, W]), in1=factor[:], op=ALU.mult)
+            return steps
+
+        def scan(steps, addend, name):
+            states = const.tile([P, N, W], F32, name="states_" + name)
+            nc.vector.tensor_tensor_scan(
+                out=states[:].rearrange("p n w -> p (n w)"), data0=steps[:].rearrange("p n w -> p (n w)"),
+                data1=addend[:].rearrange("p n w -> p (n w)"), initial=0.0, op0=ALU.mult, op1=ALU.add,
+            )
+            return states[:, :, W - 1]
 
         a0 = const.tile([P, N], F32)
         nc.vector.scalar_tensor_tensor(out=a0[:], in0=kap_bf[:], scalar=-1.0, in1=kap_bf[:], op0=ALU.mult, op1=ALU.max)
+        n_i = const.tile([P, N], I32)
+        nc.vector.tensor_scalar(out=n_i[:], in0=a0[:], scalar1=80.0, scalar2=LOG2E, op0=ALU.min, op1=ALU.mult)
         aa = const.tile([P, N], F32)
         nc.vector.tensor_scalar(out=aa[:], in0=a0[:], scalar1=80.0, scalar2=None, op0=ALU.min)
-        n_i = const.tile([P, N], I32)
-        nc.vector.tensor_scalar(out=n_i[:], in0=aa[:], scalar1=LOG2E, scalar2=None, op0=ALU.mult)
         nfl = const.tile([P, N], F32)
         nc.vector.tensor_copy(out=nfl[:], in_=n_i[:])
-        e_i = const.tile([P, N], I32)
-        nc.vector.tensor_scalar(out=e_i[:], in0=n_i[:], scalar1=-1.0, scalar2=127.0, op0=ALU.mult, op1=ALU.add)
         r1 = const.tile([P, N], F32)
         nc.vector.scalar_tensor_tensor(out=r1[:], in0=nfl[:], scalar=LN2_HI, in1=aa[:], op0=ALU.mult, op1=ALU.subtract)
-        p_i = const.tile([P, N], I32)
-        nc.vector.tensor_single_scalar(out=p_i[:], in_=e_i[:], scalar=23, op=ALU.logical_shift_left)
+        e_i = const.tile([P, N], I32)
+        nc.vector.tensor_scalar(out=e_i[:], in0=n_i[:], scalar1=-1.0, scalar2=127.0, op0=ALU.mult, op1=ALU.add)
         rr = const.tile([P, N], F32)
         nc.vector.scalar_tensor_tensor(out=rr[:], in0=nfl[:], scalar=LN2_LO, in1=r1[:], op0=ALU.mult, op1=ALU.add)
-        er = series(rr, coef_e, W, "exp")
+        p_i = const.tile([P, N], I32)
+        nc.vector.tensor_single_scalar(out=p_i[:], in_=e_i[:], scalar=23, op=ALU.logical_shift_left)
+        er = scan(series(rr, step_e, unit, "exp"), unit, "exp")
         yy = const.tile([P, N], F32)
         nc.vector.tensor_tensor(out=yy[:], in0=er, in1=p_i[:].bitcast(F32), op=ALU.mult)
         dd = const.tile([P, N], F32)
@@ -184,17 +190,18 @@ def tile_weightedaggregation_t_kernel(tc, x_aug, t, t_left, t_right, kappa, out)
         nc.vector.reciprocal(out=rd[:], in_=dd[:])
         ss = const.tile([P, N], F32)
         nc.vector.tensor_tensor(out=ss[:], in0=yy[:], in1=rd[:], op=ALU.mult)
-        l1p = series(ss, coef_l, WL, "log")
+        l1p = scan(series(ss, first, coef_l, "log"), coef_l, "log")
         kk = const.tile([P, N], F32)
         nc.vector.scalar_tensor_tensor(out=kk[:], in0=kap_bf[:], scalar=0.0, in1=l1p, op0=ALU.max, op1=ALU.add)
         rk = const.tile([P, N], F32)
         nc.vector.reciprocal(out=rk[:], in_=kk[:])
+        b_l = const.tile([P, N, MT], F32)
+        nc.vector.scalar_tensor_tensor(out=b_l[:], in0=tlq[:], scalar=-1.0, in1=rk[:].unsqueeze(2).to_broadcast([P, N, MT]),
+                                       op0=ALU.mult, op1=ALU.mult)
         nrk = const.tile([P, N], F32)
         nc.vector.tensor_scalar(out=nrk[:], in0=rk[:], scalar1=-1.0, scalar2=None, op0=ALU.mult)
         b_r = const.tile([P, N, MT], F32)
         nc.vector.tensor_tensor(out=b_r[:], in0=trq[:], in1=rk[:].unsqueeze(2).to_broadcast([P, N, MT]), op=ALU.mult)
-        b_l = const.tile([P, N, MT], F32)
-        nc.vector.tensor_tensor(out=b_l[:], in0=tlq[:], in1=nrk[:].unsqueeze(2).to_broadcast([P, N, MT]), op=ALU.mult)
 
         dsum = const.tile([P, N, MT], F32)
         dse = const.tile([P, N, MT], F32)
@@ -212,10 +219,10 @@ def tile_weightedaggregation_t_kernel(tc, x_aug, t, t_left, t_right, kappa, out)
             s1 = sgp.tile([P, L], F32, name="s1")
             s2 = sgp.tile([P, L], F32, name="s2")
             st[("s", q)] = (s1, s2)
-            nc.scalar.activation(out=s1[:], in_=t_all[:], func=ACT.Sigmoid,
-                                 bias=b_r[:, n, mt:mt + 1], scale=nrk[:, n:n + 1])
             nc.scalar.activation(out=s2[:], in_=t_all[:], func=ACT.Sigmoid,
                                  bias=b_l[:, n, mt:mt + 1], scale=rk[:, n:n + 1])
+            nc.scalar.activation(out=s1[:], in_=t_all[:], func=ACT.Sigmoid,
+                                 bias=b_r[:, n, mt:mt + 1], scale=nrk[:, n:n + 1])
 
         def prod(q):
             n, mt = divmod(q, MT)

@@ -143,12 +143,13 @@ def tile_weightedaggregation_t_kernel(tc, x_aug, t, t_left, t_right, kappa, out)
         for c in range(PASSES):
             bank = turnp.tile([P, K_PASS], F32, name="turn")
             nc.tensor.matmul(
-                out=bank[:].rearrange("q (u p e) -> q u p e", u=2, e=2),
+                out=bank[:],
                 lhsT=ident_bf[:, 0:1].to_broadcast([P, P]),
-                rhs=trow[:, c * K_PASS:(c + 1) * K_PASS].rearrange("r (p u e) -> r u p e", u=2, e=2),
+                rhs=trow[:, c * K_PASS:(c + 1) * K_PASS],
                 start=True, stop=True,
             )
-            nc.scalar.copy(out=t_all[:, c * K_PASS:(c + 1) * K_PASS], in_=bank[:])
+            nc.scalar.copy(out=t_all[:, c * K_PASS:(c + 1) * K_PASS].rearrange("q (u p e) -> q u p e", u=2, e=2),
+                           in_=bank[:].rearrange("q (p u e) -> q u p e", u=2, e=2))
 
         regroup(0, True)
 
@@ -181,15 +182,17 @@ def tile_weightedaggregation_t_kernel(tc, x_aug, t, t_left, t_right, kappa, out)
         nc.vector.scalar_tensor_tensor(out=rr[:], in0=nfl[:], scalar=LN2_LO, in1=r1[:], op0=ALU.mult, op1=ALU.add)
         p_i = const.tile([P, N], I32)
         nc.vector.tensor_single_scalar(out=p_i[:], in_=e_i[:], scalar=23, op=ALU.logical_shift_left)
-        er = scan(series(rr, step_e, unit, "exp"), unit, "exp")
-        yy = const.tile([P, N], F32)
-        nc.vector.tensor_tensor(out=yy[:], in0=er, in1=p_i[:].bitcast(F32), op=ALU.mult)
+        steps_e = series(rr, step_e, unit, "exp")
+        scaled = const.tile([P, N, W], F32)
+        nc.vector.tensor_tensor(out=scaled[:], in0=p_i[:].bitcast(F32).unsqueeze(2).to_broadcast([P, N, W]), in1=unit[:],
+                                op=ALU.mult)
+        yy = scan(steps_e, scaled, "exp")
         dd = const.tile([P, N], F32)
-        nc.vector.tensor_scalar(out=dd[:], in0=yy[:], scalar1=2.0, scalar2=None, op0=ALU.add)
+        nc.vector.tensor_scalar(out=dd[:], in0=yy, scalar1=2.0, scalar2=None, op0=ALU.add)
         rd = const.tile([P, N], F32)
         nc.vector.reciprocal(out=rd[:], in_=dd[:])
         ss = const.tile([P, N], F32)
-        nc.vector.tensor_tensor(out=ss[:], in0=yy[:], in1=rd[:], op=ALU.mult)
+        nc.vector.tensor_tensor(out=ss[:], in0=yy, in1=rd[:], op=ALU.mult)
         l1p = scan(series(ss, first, coef_l, "log"), coef_l, "log")
         kk = const.tile([P, N], F32)
         nc.vector.scalar_tensor_tensor(out=kk[:], in0=kap_bf[:], scalar=0.0, in1=l1p, op0=ALU.max, op1=ALU.add)
@@ -282,7 +285,7 @@ def tile_weightedaggregation_t_kernel(tc, x_aug, t, t_left, t_right, kappa, out)
         def store(i, o_sb, lo, count):
             n, g = divmod(i, NG)
             b0 = g * BG + lo
-            nc.scalar.dma_start(
+            nc.sync.dma_start(
                 out=out[b0:b0 + count, n, :, :].rearrange("b (p m) f -> p b (m f)", m=MT),
                 in_=o_sb[:, lo:lo + count].rearrange("p b m f -> p b (m f)"),
             )

@@ -102,6 +102,12 @@ def tile_weightedaggregation_t_kernel(tc, x_aug, t, t_left, t_right, kappa, out)
                         out=xg[:, 1].rearrange("p (b g i) j -> p b g j i", b=BG, i=8),
                         in_=raw[:, 1].rearrange("p b (j g i) -> p b g j i", j=PACK, i=8),
                     )
+            elif i == 1 and not on_scalar:
+                for c in range(PASSES):
+                    nc.vector.tensor_copy(
+                        out=xg[:, c].rearrange("p (b g i) j -> p b g j i", b=BG, i=8),
+                        in_=raw[:, c].rearrange("p b (j g i) -> p b g j i", j=PACK, i=8),
+                    )
             elif not on_scalar:
                 nc.vector.tensor_copy(
                     out=xg[:].rearrange("p c (b g i) j -> p (c b) g j i", b=BG, i=8),

@@ -26,10 +26,10 @@ NG = B // BG
 COLS = BG * F
 CHUNKS = N * NG
 PIECES = N * 4
-W = 26
+W_E = 16
+W_L = 26
 LOG2E = 1.4426950408889634
-LN2_HI = 0.693145751953125
-LN2_LO = 1.4286068203094173e-06
+LN2 = 0.6931471805599453
 
 LOAD_LEAD = 9
 SIG_LEAD = 8
@@ -121,29 +121,28 @@ def tile_weightedaggregation_t_kernel(tc, x_aug, t, t_left, t_right, kappa, out)
 
         ones = const.tile([P, 2], F32)
         nc.vector.memset(ones[:], 1.0)
-        count = const.tile([P, N, W], F32)
-        nc.gpsimd.iota(count[:].rearrange("p n w -> p (n w)"), pattern=[[0, N], [-1, W]], base=W, channel_multiplier=0,
-                       allow_small_or_imprecise_dtypes=True)
+        count = const.tile([P, W_L], F32)
+        nc.gpsimd.iota(count[:], pattern=[[-1, W_L]], base=W_L, channel_multiplier=0, allow_small_or_imprecise_dtypes=True)
         ident = const.tile([P, P], F32)
         make_identity(nc, ident[:])
         ident_bf = const.tile([P, P], BF16)
         make_identity(nc, ident_bf[:])
         warm = const.tile([P, 2], F32)
         nc.scalar.activation(out=warm[:], in_=ones[:], func=ACT.Sigmoid)
-        step_e = const.tile([P, N, W], F32)
-        nc.vector.reciprocal(out=step_e[:], in_=count[:])
-        nc.vector.memset(step_e[:, :, 0:1], 0.0)
-        unit = const.tile([P, N, W], F32)
-        nc.vector.memset(unit[:], 1.0)
-        half = const.tile([P, N, W], F32)
+        step_e = const.tile([P, W_E], F32)
+        nc.vector.reciprocal(out=step_e[:], in_=count[:, W_L - W_E:])
+        nc.vector.memset(step_e[:, 0:1], 0.0)
+        last = const.tile([P, N, W_E], F32)
+        nc.vector.memset(last[:], 0.0)
+        nc.vector.memset(last[:, :, W_E - 1:W_E], 1.0)
+        half = const.tile([P, W_L], F32)
         nc.vector.tensor_scalar(out=half[:], in0=count[:], scalar1=-1.0, scalar2=0.5, op0=ALU.add, op1=ALU.mult)
-        coef_l = const.tile([P, N, W], F32)
-        nc.vector.memset(coef_l[:], 0.0)
-        nc.vector.reciprocal(out=coef_l[:].rearrange("p n (a b) -> p n a b", b=2)[:, :, :, 0],
-                             in_=half[:].rearrange("p n (a b) -> p n a b", b=2)[:, :, :, 0])
-        first = const.tile([P, N, W], F32)
-        nc.vector.memset(first[:], 1.0)
-        nc.vector.memset(first[:, :, 0:1], 0.0)
+        coef_1 = const.tile([P, W_L], F32)
+        nc.vector.memset(coef_1[:], 0.0)
+        nc.vector.reciprocal(out=coef_1[:].rearrange("p (a b) -> p a b", b=2)[:, :, 0],
+                             in_=half[:].rearrange("p (a b) -> p a b", b=2)[:, :, 0])
+        coef_l = const.tile([P, N, W_L], F32)
+        nc.vector.tensor_copy(out=coef_l[:], in_=coef_1[:].unsqueeze(1).to_broadcast([P, N, W_L]))
 
         t_all = const.tile([P, L], BF16)
         for c in range(PASSES):
@@ -159,51 +158,40 @@ def tile_weightedaggregation_t_kernel(tc, x_aug, t, t_left, t_right, kappa, out)
 
         regroup(0, True)
 
-        def series(arg, factor, addend, name):
-            steps = const.tile([P, N, W], F32, name="steps_" + name)
-            nc.vector.tensor_tensor(out=steps[:], in0=arg[:].unsqueeze(2).to_broadcast([P, N, W]), in1=factor[:], op=ALU.mult)
-            return steps
-
-        def scan(steps, addend, name):
-            states = const.tile([P, N, W], F32, name="states_" + name)
-            nc.vector.tensor_tensor_scan(
-                out=states[:].rearrange("p n w -> p (n w)"), data0=steps[:].rearrange("p n w -> p (n w)"),
-                data1=addend[:].rearrange("p n w -> p (n w)"), initial=0.0, op0=ALU.mult, op1=ALU.add,
-            )
-            return states[:, :, W - 1]
-
         a0 = const.tile([P, N], F32)
         nc.vector.scalar_tensor_tensor(out=a0[:], in0=kap_bf[:], scalar=-1.0, in1=kap_bf[:], op0=ALU.mult, op1=ALU.max)
+        nc.vector.tensor_scalar(out=coef_l[:, :, W_L - 1], in0=kap_bf[:], scalar1=0.0, scalar2=None, op0=ALU.max)
         n_i = const.tile([P, N], I32)
         nc.vector.tensor_scalar(out=n_i[:], in0=a0[:], scalar1=80.0, scalar2=LOG2E, op0=ALU.min, op1=ALU.mult)
         aa = const.tile([P, N], F32)
         nc.vector.tensor_scalar(out=aa[:], in0=a0[:], scalar1=80.0, scalar2=None, op0=ALU.min)
-        nfl = const.tile([P, N], F32)
-        nc.vector.tensor_copy(out=nfl[:], in_=n_i[:])
-        r1 = const.tile([P, N], F32)
-        nc.vector.scalar_tensor_tensor(out=r1[:], in0=nfl[:], scalar=LN2_HI, in1=aa[:], op0=ALU.mult, op1=ALU.subtract)
         e_i = const.tile([P, N], I32)
-        nc.vector.tensor_scalar(out=e_i[:], in0=n_i[:], scalar1=-1.0, scalar2=127.0, op0=ALU.mult, op1=ALU.add)
+        nc.vector.tensor_scalar(out=e_i[:], in0=n_i[:], scalar1=128.0, scalar2=None, op0=ALU.add)
         rr = const.tile([P, N], F32)
-        nc.vector.scalar_tensor_tensor(out=rr[:], in0=nfl[:], scalar=LN2_LO, in1=r1[:], op0=ALU.mult, op1=ALU.add)
+        nc.vector.scalar_tensor_tensor(out=rr[:], in0=n_i[:], scalar=-LN2, in1=aa[:], op0=ALU.mult, op1=ALU.add)
         p_i = const.tile([P, N], I32)
         nc.vector.tensor_single_scalar(out=p_i[:], in_=e_i[:], scalar=23, op=ALU.logical_shift_left)
-        steps_e = series(rr, step_e, unit, "exp")
-        scaled = const.tile([P, N, W], F32)
-        nc.vector.tensor_tensor(out=scaled[:], in0=p_i[:].bitcast(F32).unsqueeze(2).to_broadcast([P, N, W]), in1=unit[:],
-                                op=ALU.mult)
-        yy = scan(steps_e, scaled, "exp")
-        dd = const.tile([P, N], F32)
-        nc.vector.tensor_scalar(out=dd[:], in0=yy, scalar1=2.0, scalar2=None, op0=ALU.add)
-        rd = const.tile([P, N], F32)
-        nc.vector.reciprocal(out=rd[:], in_=dd[:])
+        steps_e = const.tile([P, N, W_E], F32)
+        nc.vector.tensor_tensor(out=steps_e[:], in0=rr[:].unsqueeze(2).to_broadcast([P, N, W_E]),
+                                in1=step_e[:].unsqueeze(1).to_broadcast([P, N, W_E]), op=ALU.mult)
+        scaled = const.tile([P, N, W_E], F32)
+        nc.vector.tensor_tensor(out=scaled[:], in0=p_i[:].bitcast(F32).unsqueeze(2).to_broadcast([P, N, W_E]), in1=last[:],
+                                op=ALU.add)
+        states_e = const.tile([P, N, W_E], F32)
+        nc.vector.tensor_tensor_scan(
+            out=states_e[:].rearrange("p n w -> p (n w)"), data0=steps_e[:].rearrange("p n w -> p (n w)"),
+            data1=scaled[:].rearrange("p n w -> p (n w)"), initial=0.0, op0=ALU.mult, op1=ALU.add,
+        )
         ss = const.tile([P, N], F32)
-        nc.vector.tensor_tensor(out=ss[:], in0=yy, in1=rd[:], op=ALU.mult)
-        l1p = scan(series(ss, first, coef_l, "log"), coef_l, "log")
-        kk = const.tile([P, N], F32)
-        nc.vector.scalar_tensor_tensor(out=kk[:], in0=kap_bf[:], scalar=0.0, in1=l1p, op0=ALU.max, op1=ALU.add)
+        nc.vector.reciprocal(out=ss[:], in_=states_e[:, :, W_E - 1])
+        states_l = const.tile([P, N, W_L], F32)
+        for n in range(N):
+            nc.vector.tensor_tensor_scan(
+                out=states_l[:, n, :], data0=ss[:, n:n + 1].to_broadcast([P, W_L]), data1=coef_l[:, n, :],
+                initial=0.0, op0=ALU.mult, op1=ALU.add,
+            )
         rk = const.tile([P, N], F32)
-        nc.vector.reciprocal(out=rk[:], in_=kk[:])
+        nc.vector.reciprocal(out=rk[:], in_=states_l[:, :, W_L - 1])
         b_l = const.tile([P, N, MT], F32)
         nc.vector.scalar_tensor_tensor(out=b_l[:], in0=tlq[:], scalar=-1.0, in1=rk[:].unsqueeze(2).to_broadcast([P, N, MT]),
                                        op0=ALU.mult, op1=ALU.mult)

@@ -60,13 +60,11 @@ def tile_weightedaggregation_t_kernel(tc, x_aug, t, t_left, t_right, kappa, out)
 
         kap_bf = const.tile([P, N], BF16)
         nc.sync.dma_start(out=kap_bf[:], in_=kappa.rearrange("n o -> (n o)").partition_broadcast(P))
-        trow = const.tile([P, L], BF16)
-        nc.vector.memset(trow[:], 0.0)
-        nc.sync.dma_start(out=trow[0:1, :], in_=t.rearrange("l o -> o l"))
-        trq = const.tile([P, N, MT], BF16)
-        nc.sync.dma_start(out=trq[:], in_=t_right.rearrange("n (q j) -> q n j", j=MT))
-        tlq = const.tile([P, N, MT], BF16)
-        nc.sync.dma_start(out=tlq[:], in_=t_left.rearrange("n (q j) -> q n j", j=MT))
+        rows = const.tile([P, L + M], BF16)
+        nc.vector.memset(rows[:].bitcast(U32), 0)
+        nc.sync.dma_start(out=rows[0:1, :L], in_=t.rearrange("l o -> o l"))
+        nc.sync.dma_start(out=rows[0:N, L:], in_=t_left)
+        nc.sync.dma_start(out=rows[N:2 * N, L:], in_=t_right)
 
         raws = {}
         xgs = {}
@@ -150,11 +148,16 @@ def tile_weightedaggregation_t_kernel(tc, x_aug, t, t_left, t_right, kappa, out)
             nc.tensor.matmul(
                 out=bank[:],
                 lhsT=ident_bf[:, 0:1].to_broadcast([P, P]),
-                rhs=trow[:, c * K_PASS:(c + 1) * K_PASS],
+                rhs=rows[:, c * K_PASS:(c + 1) * K_PASS],
                 start=True, stop=True,
             )
             nc.scalar.copy(out=t_all[:, c * K_PASS:(c + 1) * K_PASS].rearrange("q (u p e) -> q u p e", u=2, e=2),
                            in_=bank[:].rearrange("q (p u e) -> q u p e", u=2, e=2))
+
+        edges = accp.tile([P, MT, P], BF16, name="acc")
+        for mt in range(MT):
+            nc.tensor.transpose(edges[:, mt, :], rows[:, L + mt:L + M:MT], ident_bf[:])
+        edges_n = edges[:].rearrange("q m r -> q r m")
 
         regroup(0, True)
 
@@ -193,12 +196,12 @@ def tile_weightedaggregation_t_kernel(tc, x_aug, t, t_left, t_right, kappa, out)
         rk = const.tile([P, N], F32)
         nc.vector.reciprocal(out=rk[:], in_=states_l[:, :, W_L - 1])
         b_l = const.tile([P, N, MT], F32)
-        nc.vector.scalar_tensor_tensor(out=b_l[:], in0=tlq[:], scalar=-1.0, in1=rk[:].unsqueeze(2).to_broadcast([P, N, MT]),
+        nc.vector.scalar_tensor_tensor(out=b_l[:], in0=edges_n[:, 0:N], scalar=-1.0, in1=rk[:].unsqueeze(2).to_broadcast([P, N, MT]),
                                        op0=ALU.mult, op1=ALU.mult)
         nrk = const.tile([P, N], F32)
         nc.vector.tensor_scalar(out=nrk[:], in0=rk[:], scalar1=-1.0, scalar2=None, op0=ALU.mult)
         b_r = const.tile([P, N, MT], F32)
-        nc.vector.tensor_tensor(out=b_r[:], in0=trq[:], in1=rk[:].unsqueeze(2).to_broadcast([P, N, MT]), op=ALU.mult)
+        nc.vector.tensor_tensor(out=b_r[:], in0=edges_n[:, N:2 * N], in1=rk[:].unsqueeze(2).to_broadcast([P, N, MT]), op=ALU.mult)
 
         dsum = const.tile([P, N, MT], F32)
         dse = const.tile([P, N, MT], F32)

@@ -38,7 +38,7 @@ TURN_LEAD = 6
 XR_LEAD = 4
 XQ_LEAD = 3
 RAW_BUFS = 7
-RUNS = 4
+HALF = 4
 
 FLOPS = 2 * B * N * M * L * F
 
@@ -112,7 +112,7 @@ def tile_weightedaggregation_t_kernel(tc, x_aug, t, t_left, t_right, kappa, out)
                     in_=raw[:].rearrange("p c b (j g i) -> p (c b) g j i", j=PACK, i=8),
                 )
 
-        S_REGROUP = (0,)
+        S_REGROUP = (0, 11)
 
         for i in range(RAW_BUFS):
             load(i)
@@ -262,6 +262,49 @@ def tile_weightedaggregation_t_kernel(tc, x_aug, t, t_left, t_right, kappa, out)
             else:
                 nc.vector.reciprocal(out=rden[:, n, :], in_=dse[:, n, :])
 
+        def regroup_last(i):
+            raw = raws[i]
+            xg = xgp.tile([P, BG // HALF, PASSES, HALF * F, PACK], BF16, name="xg", align_bytes=64)
+            xgs[i] = xg
+            for h in range(BG // HALF):
+                for c in range(PASSES):
+                    nc.vector.tensor_copy(
+                        out=xg[:, h, c].rearrange("p (b g i) j -> p b g j i", b=HALF, i=8),
+                        in_=raw[:, c, h * HALF:(h + 1) * HALF].rearrange("p b (j g i) -> p b g j i", j=PACK, i=8),
+                    )
+
+        def quant_last(i):
+            xg = xgs[i]
+            xc = xcp.tile([P, BG // HALF, PASSES, HALF * F], U32, name="xc", align_bytes=64)
+            xs = xcp.tile([P, BG // HALF, PASSES, HALF * F], U8, name="xs", align_bytes=64)
+            for h in range(BG // HALF):
+                nc.vector.quantize_mx(
+                    out=xc[:, h].rearrange("p c w -> p (c w)").bitcast(FP8X4),
+                    scales=xs[:, h].rearrange("p c w -> p (c w)"),
+                    in_=xg[:, h].rearrange("p c w j -> p (c w j)"),
+                )
+            xqs[i] = (xc, xs)
+
+        def multiply_last(i):
+            n, g = divmod(i, NG)
+            xc, xs = xqs[i]
+            o_sb = outp.tile([P, BG, MT, F], F32, name="o_sb")
+            for h in range(BG // HALF):
+                for mt in range(MT):
+                    acc = accp.tile([P, HALF * F], F32, name="acc")
+                    for c in range(PASSES):
+                        nc.tensor.matmul_mx(
+                            out=acc[:],
+                            lhsT=a_codes[n][:, c, mt * P:(mt + 1) * P].bitcast(FP8X4),
+                            lhsT_scale=a_scales[n][:, c, mt * P:(mt + 1) * P],
+                            rhs=xc[:, h, c, :].bitcast(FP8X4),
+                            rhs_scale=xs[:, h, c, :],
+                            start=(c == 0), stop=(c == PASSES - 1),
+                        )
+                    evacuate(mt % 2 == 1, o_sb[:, h * HALF:(h + 1) * HALF, mt, :],
+                             acc[:].rearrange("p (b f) -> p b f", f=F), n, mt)
+                store(i, o_sb, h * HALF, HALF)
+
         def quant(i):
             xg = xgs[i]
             xc = xcp.tile([P, PASSES, COLS], U32, name="xc", align_bytes=64)
@@ -291,11 +334,8 @@ def tile_weightedaggregation_t_kernel(tc, x_aug, t, t_left, t_right, kappa, out)
             n, g = divmod(i, NG)
             xc, xs = xqs[i]
             o_sb = outp.tile([P, BG, MT, F], F32, name="o_sb")
-            last = i == CHUNKS - 1
-            accs = []
             for mt in range(MT):
                 acc = accp.tile([P, COLS], F32, name="acc")
-                accs.append(acc)
                 for c in range(PASSES):
                     nc.tensor.matmul_mx(
                         out=acc[:],
@@ -305,18 +345,9 @@ def tile_weightedaggregation_t_kernel(tc, x_aug, t, t_left, t_right, kappa, out)
                         rhs_scale=xs[:, c, :],
                         start=(c == 0), stop=(c == PASSES - 1),
                     )
-                if not last:
-                    evacuate(False, o_sb[:, :, mt, :],
-                             acc[:].rearrange("p (b f) -> p b f", f=F), n, mt)
-            if last:
-                for bh in range(BG // RUNS):
-                    for mt in range(MT):
-                        evacuate(mt % 2 == 1, o_sb[:, bh * RUNS:(bh + 1) * RUNS, mt, :],
-                                 accs[mt][:, bh * RUNS * F:(bh + 1) * RUNS * F].rearrange("p (b f) -> p b f", f=F),
-                                 n, mt)
-                    store(i, o_sb, bh * RUNS, RUNS)
-            else:
-                store(i, o_sb, 0, BG)
+                evacuate(False, o_sb[:, :, mt, :],
+                         acc[:].rearrange("p (b f) -> p b f", f=F), n, mt)
+            store(i, o_sb, 0, BG)
 
         done_r = set()
         done_q = set()
@@ -324,12 +355,18 @@ def tile_weightedaggregation_t_kernel(tc, x_aug, t, t_left, t_right, kappa, out)
         def do_regroup(i):
             if 0 <= i < CHUNKS and i not in done_r:
                 done_r.add(i)
-                regroup(i, False)
+                if i == CHUNKS - 1:
+                    regroup_last(i)
+                else:
+                    regroup(i, False)
 
         def do_quant(i):
             if 0 <= i < CHUNKS and i not in done_q:
                 done_q.add(i)
-                quant(i)
+                if i == CHUNKS - 1:
+                    quant_last(i)
+                else:
+                    quant(i)
 
         for p in range(-SIG_LEAD, CHUNKS):
             if RAW_BUFS <= p + LOAD_LEAD < CHUNKS:
@@ -342,8 +379,12 @@ def tile_weightedaggregation_t_kernel(tc, x_aug, t, t_left, t_right, kappa, out)
                 sig(p + SIG_LEAD)
             if 0 <= qt < PIECES:
                 take(qt)
-            if p >= 0:
+            if p == CHUNKS - 1:
+                multiply_last(p)
+            elif p >= 0:
                 multiply(p)
+            if p == 6:
+                regroup(11, True)
             r_due = 0 <= qt < PIECES and qt % MT == MT - 1
             if r_due:
                 rden_step(qt // MT, 0)

@@ -61,7 +61,8 @@ def tile_weightedaggregation_t_kernel(tc, x_aug, t, t_left, t_right, kappa, out)
         kap_bf = const.tile([P, N], BF16)
         nc.sync.dma_start(out=kap_bf[:], in_=kappa.rearrange("n o -> (n o)").partition_broadcast(P))
         rows = const.tile([P, L + M], BF16)
-        nc.vector.memset(rows[:].bitcast(U32), 0)
+        nc.vector.memset(rows[:, :L].bitcast(U32), 0)
+        nc.gpsimd.memset(rows[:, L:].bitcast(U32), 0)
         nc.sync.dma_start(out=rows[0:1, :L], in_=t.rearrange("l o -> o l"))
         nc.sync.dma_start(out=rows[0:N, L:], in_=t_left)
         nc.sync.dma_start(out=rows[N:2 * N, L:], in_=t_right)
@@ -83,36 +84,23 @@ def tile_weightedaggregation_t_kernel(tc, x_aug, t, t_left, t_right, kappa, out)
                 )
             raws[i] = raw
 
-        def regroup(i, on_scalar):
-            raw = raws[i]
+        def group_tile(i):
             if i not in xgs:
                 xg = xgp.tile([P, PASSES, COLS, PACK], BF16, name="xg", align_bytes=64)
                 xgs[i] = xg
-            xg = xgs[i]
-            if i in S_REGROUP:
-                if on_scalar:
-                    nc.scalar.copy(
-                        out=xg[:, 0].rearrange("p (b f) j -> p b f j", b=BG),
-                        in_=raw[:, 0].rearrange("p b (j f) -> p b f j", j=PACK),
-                    )
-                else:
-                    nc.vector.tensor_copy(
-                        out=xg[:, 1].rearrange("p (b g i) j -> p b g j i", b=BG, i=8),
-                        in_=raw[:, 1].rearrange("p b (j g i) -> p b g j i", j=PACK, i=8),
-                    )
-            elif i == 1 and not on_scalar:
-                for c in range(PASSES):
-                    nc.vector.tensor_copy(
-                        out=xg[:, c].rearrange("p (b g i) j -> p b g j i", b=BG, i=8),
-                        in_=raw[:, c].rearrange("p b (j g i) -> p b g j i", j=PACK, i=8),
-                    )
-            elif not on_scalar:
-                nc.vector.tensor_copy(
-                    out=xg[:].rearrange("p c (b g i) j -> p (c b) g j i", b=BG, i=8),
-                    in_=raw[:].rearrange("p c b (j g i) -> p (c b) g j i", j=PACK, i=8),
-                )
+            return xgs[i]
 
-        S_REGROUP = (0, 11)
+        def regroup_pass(i, c):
+            nc.vector.tensor_copy(
+                out=group_tile(i)[:, c].rearrange("p (b g i) j -> p b g j i", b=BG, i=8),
+                in_=raws[i][:, c].rearrange("p b (j g i) -> p b g j i", j=PACK, i=8),
+            )
+
+        def regroup(i):
+            nc.vector.tensor_copy(
+                out=group_tile(i)[:].rearrange("p c (b g i) j -> p (c b) g j i", b=BG, i=8),
+                in_=raws[i][:].rearrange("p c b (j g i) -> p (c b) g j i", j=PACK, i=8),
+            )
 
         for i in range(RAW_BUFS):
             load(i)
@@ -158,8 +146,6 @@ def tile_weightedaggregation_t_kernel(tc, x_aug, t, t_left, t_right, kappa, out)
         for mt in range(MT):
             nc.tensor.transpose(edges[:, mt, :], rows[:, L + mt:L + M:MT], ident_bf[:])
         edges_n = edges[:].rearrange("q m r -> q r m")
-
-        regroup(0, True)
 
         a0 = const.tile([P, N], F32)
         nc.vector.scalar_tensor_tensor(out=a0[:], in0=kap_bf[:], scalar=-1.0, in1=kap_bf[:], op0=ALU.mult, op1=ALU.max)
@@ -349,8 +335,15 @@ def tile_weightedaggregation_t_kernel(tc, x_aug, t, t_left, t_right, kappa, out)
                          acc[:].rearrange("p (b f) -> p b f", f=F), n, mt)
             store(i, o_sb, 0, BG)
 
-        done_r = set()
-        done_q = set()
+        ahead = {-7: [(regroup_pass, 0, 0), (regroup_pass, 0, 1)]}
+        behind = {
+            -7: [(regroup_pass, 1, 0), (quant, 0)],
+            -6: [(regroup_pass, 1, 1)],
+            -5: [(regroup_pass, 2, 0), (quant, 1)],
+            -4: [(regroup_pass, 2, 1)],
+        }
+        done_r = {0, 1, 2}
+        done_q = {0, 1}
 
         def do_regroup(i):
             if 0 <= i < CHUNKS and i not in done_r:
@@ -358,7 +351,7 @@ def tile_weightedaggregation_t_kernel(tc, x_aug, t, t_left, t_right, kappa, out)
                 if i == CHUNKS - 1:
                     regroup_last(i)
                 else:
-                    regroup(i, False)
+                    regroup(i)
 
         def do_quant(i):
             if 0 <= i < CHUNKS and i not in done_q:
@@ -383,21 +376,15 @@ def tile_weightedaggregation_t_kernel(tc, x_aug, t, t_left, t_right, kappa, out)
                 multiply_last(p)
             elif p >= 0:
                 multiply(p)
-            if p == 6:
-                regroup(11, True)
             r_due = 0 <= qt < PIECES and qt % MT == MT - 1
             if r_due:
                 rden_step(qt // MT, 0)
-            if p == -7:
-                do_regroup(0)
-                do_regroup(1)
-                do_quant(0)
-            if p == -6:
-                do_regroup(2)
-            if p == -5:
-                do_quant(1)
+            for work in ahead.get(p, []):
+                work[0](*work[1:])
             if 0 <= q < PIECES:
                 prod(q)
+            for work in behind.get(p, []):
+                work[0](*work[1:])
             if r_due:
                 rden_step(qt // MT, 1)
             do_quant(p + XQ_LEAD)

@@ -39,6 +39,8 @@ XR_LEAD = 4
 XQ_LEAD = 3
 RAW_BUFS = 7
 HALF = 4
+SHARED = 10
+SHARED_LEAD = 5
 
 FLOPS = 2 * B * N * M * L * F
 
@@ -94,6 +96,12 @@ def tile_weightedaggregation_t_kernel(tc, x_aug, t, t_left, t_right, kappa, out)
             nc.vector.tensor_copy(
                 out=group_tile(i)[:, c].rearrange("p (b g i) j -> p b g j i", b=BG, i=8),
                 in_=raws[i][:, c].rearrange("p b (j g i) -> p b g j i", j=PACK, i=8),
+            )
+
+        def regroup_on_scalar(i, c):
+            nc.scalar.copy(
+                out=group_tile(i)[:, c].rearrange("p (b f) j -> p b f j", b=BG),
+                in_=raws[i][:, c].rearrange("p b (j f) -> p b f j", j=PACK),
             )
 
         def regroup(i):
@@ -350,6 +358,8 @@ def tile_weightedaggregation_t_kernel(tc, x_aug, t, t_left, t_right, kappa, out)
                 done_r.add(i)
                 if i == CHUNKS - 1:
                     regroup_last(i)
+                elif i == SHARED:
+                    regroup_pass(i, 1)
                 else:
                     regroup(i)
 
@@ -376,6 +386,8 @@ def tile_weightedaggregation_t_kernel(tc, x_aug, t, t_left, t_right, kappa, out)
                 multiply_last(p)
             elif p >= 0:
                 multiply(p)
+            if p + SHARED_LEAD == SHARED:
+                regroup_on_scalar(SHARED, 0)
             r_due = 0 <= qt < PIECES and qt % MT == MT - 1
             if r_due:
                 rden_step(qt // MT, 0)

from contextlib import ExitStack

import concourse.mybir as mybir
from concourse.masks import make_identity

F32 = mybir.dt.float32
BF16 = mybir.dt.bfloat16
I32 = mybir.dt.int32
U32 = mybir.dt.uint32
U8 = mybir.dt.uint8
FP8X4 = mybir.dt.float8_e4m3fn_x4
ACT = mybir.ActivationFunctionType
ALU = mybir.AluOpType
AX = mybir.AxisListType

B, N, L, M, F = 32, 4, 1024, 512, 64
EPS = 1e-8
P = 128
PACK = 4
K_PASS = P * PACK
PASSES = L // K_PASS
CJ = PASSES * PACK
MT = M // P
BG = 8
NG = B // BG
COLS = BG * F
CHUNKS = N * NG
PIECES = N * 4
W_E = 16
W_L = 26
LOG2E = 1.4426950408889634
LN2 = 0.6931471805599453

LOAD_LEAD = 9
SIG_LEAD = 8
PROD_LEAD = 7
TURN_LEAD = 6
XR_LEAD = 4
XQ_LEAD = 3
RAW_BUFS = 7
HALF = 4
SHARED = 10
SHARED_LEAD = 5

FLOPS = 2 * B * N * M * L * F


def tile_weightedaggregation_t_kernel(tc, x_aug, t, t_left, t_right, kappa, out):
    nc = tc.nc
    with ExitStack() as ctx:
        const = ctx.enter_context(tc.tile_pool(name="const", bufs=1))
        rawp = ctx.enter_context(tc.tile_pool(name="rawp", bufs=RAW_BUFS))
        xgp = ctx.enter_context(tc.tile_pool(name="xgp", bufs=4))
        xcp = ctx.enter_context(tc.tile_pool(name="xcp", bufs=5))
        outp = ctx.enter_context(tc.tile_pool(name="outp", bufs=5))
        sgp = ctx.enter_context(tc.tile_pool(name="sgp", bufs=3))
        atp = ctx.enter_context(tc.tile_pool(name="atp", bufs=3))
        gp = ctx.enter_context(tc.tile_pool(name="gp", bufs=2))
        accp = ctx.enter_context(tc.psum_pool(name="accp", bufs=6))
        turnp = ctx.enter_context(tc.psum_pool(name="turnp", bufs=2))
        ctx.enter_context(tc.manual_schedule())

        kap_bf = const.tile([P, N], BF16)
        nc.sync.dma_start(out=kap_bf[:], in_=kappa.rearrange("n o -> (n o)").partition_broadcast(P))
        rows = const.tile([P, L + M], BF16)
        nc.vector.memset(rows[:, :L].bitcast(U32), 0)
        nc.gpsimd.memset(rows[:, L:].bitcast(U32), 0)
        nc.sync.dma_start(out=rows[0:1, :L], in_=t.rearrange("l o -> o l"))
        nc.sync.dma_start(out=rows[0:N, L:], in_=t_left)
        nc.sync.dma_start(out=rows[N:2 * N, L:], in_=t_right)

        raws = {}
        xgs = {}
        xqs = {}
        st = {}

        def load(i):
            n, g = divmod(i, NG)
            raw = rawp.tile([P, PASSES, BG, PACK * F], BF16, name="raw")
            for c in range(PASSES):
                nc.sync.dma_start(
                    out=raw[:, c],
                    in_=x_aug[g * BG:(g + 1) * BG, n, c * K_PASS:(c + 1) * K_PASS, :].rearrange(
                        "b (p j) f -> p b (j f)", j=PACK
                    ),
                )
            raws[i] = raw

        def group_tile(i):
            if i not in xgs:
                xg = xgp.tile([P, PASSES, COLS, PACK], BF16, name="xg", align_bytes=64)
                xgs[i] = xg
            return xgs[i]

        def regroup_pass(i, c):
            nc.vector.tensor_copy(
                out=group_tile(i)[:, c].rearrange("p (b g i) j -> p b g j i", b=BG, i=8),
                in_=raws[i][:, c].rearrange("p b (j g i) -> p b g j i", j=PACK, i=8),
            )

        def regroup_on_scalar(i, c):
            nc.scalar.copy(
                out=group_tile(i)[:, c].rearrange("p (b f) j -> p b f j", b=BG),
                in_=raws[i][:, c].rearrange("p b (j f) -> p b f j", j=PACK),
            )

        def regroup(i):
            nc.vector.tensor_copy(
                out=group_tile(i)[:].rearrange("p c (b g i) j -> p (c b) g j i", b=BG, i=8),
                in_=raws[i][:].rearrange("p c b (j g i) -> p (c b) g j i", j=PACK, i=8),
            )

        for i in range(RAW_BUFS):
            load(i)

        ones = const.tile([P, 2], F32)
        nc.vector.memset(ones[:], 1.0)
        count = const.tile([P, W_L], F32)
        nc.gpsimd.iota(count[:], pattern=[[-1, W_L]], base=W_L, channel_multiplier=0, allow_small_or_imprecise_dtypes=True)
        ident = const.tile([P, P], F32)
        make_identity(nc, ident[:])
        ident_bf = const.tile([P, P], BF16)
        make_identity(nc, ident_bf[:])
        warm = const.tile([P, 2], F32)
        nc.scalar.activation(out=warm[:], in_=ones[:], func=ACT.Sigmoid)
        step_e = const.tile([P, W_E], F32)
        nc.vector.reciprocal(out=step_e[:], in_=count[:, W_L - W_E:])
        nc.vector.memset(step_e[:, 0:1], 0.0)
        last = const.tile([P, N, W_E], F32)
        nc.vector.memset(last[:], 0.0)
        nc.vector.memset(last[:, :, W_E - 1:W_E], 1.0)
        half = const.tile([P, W_L], F32)
        nc.vector.tensor_scalar(out=half[:], in0=count[:], scalar1=-1.0, scalar2=0.5, op0=ALU.add, op1=ALU.mult)
        coef_1 = const.tile([P, W_L], F32)
        nc.vector.memset(coef_1[:], 0.0)
        nc.vector.reciprocal(out=coef_1[:].rearrange("p (a b) -> p a b", b=2)[:, :, 0],
                             in_=half[:].rearrange("p (a b) -> p a b", b=2)[:, :, 0])
        coef_l = const.tile([P, N, W_L], F32)
        nc.vector.tensor_copy(out=coef_l[:], in_=coef_1[:].unsqueeze(1).to_broadcast([P, N, W_L]))

        t_all = const.tile([P, L], BF16)
        for c in range(PASSES):
            bank = turnp.tile([P, K_PASS], F32, name="turn")
            nc.tensor.matmul(
                out=bank[:],
                lhsT=ident_bf[:, 0:1].to_broadcast([P, P]),
                rhs=rows[:, c * K_PASS:(c + 1) * K_PASS],
                start=True, stop=True,
            )
            nc.scalar.copy(out=t_all[:, c * K_PASS:(c + 1) * K_PASS].rearrange("q (u p e) -> q u p e", u=2, e=2),
                           in_=bank[:].rearrange("q (p u e) -> q u p e", u=2, e=2))

        edges = accp.tile([P, MT, P], BF16, name="acc")
        for mt in range(MT):
            nc.tensor.transpose(edges[:, mt, :], rows[:, L + mt:L + M:MT], ident_bf[:])
        edges_n = edges[:].rearrange("q m r -> q r m")

        a0 = const.tile([P, N], F32)
        nc.vector.scalar_tensor_tensor(out=a0[:], in0=kap_bf[:], scalar=-1.0, in1=kap_bf[:], op0=ALU.mult, op1=ALU.max)
        nc.vector.tensor_scalar(out=coef_l[:, :, W_L - 1], in0=kap_bf[:], scalar1=0.0, scalar2=None, op0=ALU.max)
        n_i = const.tile([P, N], I32)
        nc.vector.tensor_scalar(out=n_i[:], in0=a0[:], scalar1=80.0, scalar2=LOG2E, op0=ALU.min, op1=ALU.mult)
        aa = const.tile([P, N], F32)
        nc.vector.tensor_scalar(out=aa[:], in0=a0[:], scalar1=80.0, scalar2=None, op0=ALU.min)
        e_i = const.tile([P, N], I32)
        nc.vector.tensor_scalar(out=e_i[:], in0=n_i[:], scalar1=128.0, scalar2=None, op0=ALU.add)
        rr = const.tile([P, N], F32)
        nc.vector.scalar_tensor_tensor(out=rr[:], in0=n_i[:], scalar=-LN2, in1=aa[:], op0=ALU.mult, op1=ALU.add)
        p_i = const.tile([P, N], I32)
        nc.vector.tensor_single_scalar(out=p_i[:], in_=e_i[:], scalar=23, op=ALU.logical_shift_left)
        steps_e = const.tile([P, N, W_E], F32)
        nc.vector.tensor_tensor(out=steps_e[:], in0=rr[:].unsqueeze(2).to_broadcast([P, N, W_E]),
                                in1=step_e[:].unsqueeze(1).to_broadcast([P, N, W_E]), op=ALU.mult)
        scaled = const.tile([P, N, W_E], F32)
        nc.vector.tensor_tensor(out=scaled[:], in0=p_i[:].bitcast(F32).unsqueeze(2).to_broadcast([P, N, W_E]), in1=last[:],
                                op=ALU.add)
        states_e = const.tile([P, N, W_E], F32)
        nc.vector.tensor_tensor_scan(
            out=states_e[:].rearrange("p n w -> p (n w)"), data0=steps_e[:].rearrange("p n w -> p (n w)"),
            data1=scaled[:].rearrange("p n w -> p (n w)"), initial=0.0, op0=ALU.mult, op1=ALU.add,
        )
        ss = const.tile([P, N], F32)
        nc.vector.reciprocal(out=ss[:], in_=states_e[:, :, W_E - 1])
        states_l = const.tile([P, N, W_L], F32)
        for n in range(N):
            nc.vector.tensor_tensor_scan(
                out=states_l[:, n, :], data0=ss[:, n:n + 1].to_broadcast([P, W_L]), data1=coef_l[:, n, :],
                initial=0.0, op0=ALU.mult, op1=ALU.add,
            )
        rk = const.tile([P, N], F32)
        nc.vector.reciprocal(out=rk[:], in_=states_l[:, :, W_L - 1])
        b_l = const.tile([P, N, MT], F32)
        nc.vector.scalar_tensor_tensor(out=b_l[:], in0=edges_n[:, 0:N], scalar=-1.0, in1=rk[:].unsqueeze(2).to_broadcast([P, N, MT]),
                                       op0=ALU.mult, op1=ALU.mult)
        nrk = const.tile([P, N], F32)
        nc.vector.tensor_scalar(out=nrk[:], in0=rk[:], scalar1=-1.0, scalar2=None, op0=ALU.mult)
        b_r = const.tile([P, N, MT], F32)
        nc.vector.tensor_tensor(out=b_r[:], in0=edges_n[:, N:2 * N], in1=rk[:].unsqueeze(2).to_broadcast([P, N, MT]), op=ALU.mult)

        dsum = const.tile([P, N, MT], F32)
        dse = const.tile([P, N, MT], F32)
        rden = const.tile([P, N, MT], F32)
        a_codes = []
        a_scales = []
        for n in range(N):
            ac = const.tile([P, PASSES, M], U32, name="ac%d" % n, align_bytes=64)
            asc = const.tile([P, PASSES, M], U8, name="as%d" % n, align_bytes=64)
            a_codes.append(ac)
            a_scales.append(asc)

        def sig(q):
            n, mt = divmod(q, MT)
            s1 = sgp.tile([P, L], F32, name="s1")
            s2 = sgp.tile([P, L], F32, name="s2")
            st[("s", q)] = (s1, s2)
            nc.scalar.activation(out=s2[:], in_=t_all[:], func=ACT.Sigmoid,
                                 bias=b_l[:, n, mt:mt + 1], scale=rk[:, n:n + 1])
            nc.scalar.activation(out=s1[:], in_=t_all[:], func=ACT.Sigmoid,
                                 bias=b_r[:, n, mt:mt + 1], scale=nrk[:, n:n + 1])

        def prod(q):
            n, mt = divmod(q, MT)
            s1, s2 = st[("s", q)]
            a_t = atp.tile([P, L], BF16, name="a_t")
            st[("a", q)] = a_t
            nc.vector.scalar_tensor_tensor(out=a_t[:], in0=s1[:], scalar=1.0, in1=s2[:], op0=ALU.mult, op1=ALU.mult,
                                           accum_out=dsum[:, n, mt:mt + 1])

        def turn(q):
            words = st[("a", q)][:].bitcast(F32)
            bank = turnp.tile([P, PACK, P], F32, name="turn")
            st[("t", q)] = bank
            for cu in range(PACK):
                nc.tensor.transpose(bank[:, cu, :], words[:, cu * P:(cu + 1) * P], ident[:])

        def take(q):
            n, mt = divmod(q, MT)
            if mt == 0:
                grp = gp.tile([P, PASSES, M, PACK], BF16, name="grp", align_bytes=64)
                st[("g", n)] = grp
            g_words = st[("g", n)][:].rearrange("p c w j -> p (c w j)").bitcast(F32).rearrange(
                "p (c w u) -> p c w u", c=PASSES, u=2)
            nc.scalar.copy(out=g_words[:, :, mt * P:(mt + 1) * P, :],
                           in_=st[("t", q)][:].rearrange("p (c u) w -> p c w u", u=2))

        def qa(n):
            nc.vector.quantize_mx(
                out=a_codes[n][:].rearrange("p c w -> p (c w)").bitcast(FP8X4),
                scales=a_scales[n][:].rearrange("p c w -> p (c w)"),
                in_=st[("g", n)][:].rearrange("p c w j -> p (c w j)"),
            )

        def rden_step(n, step):
            if step == 0:
                nc.vector.tensor_scalar(out=dse[:, n, :], in0=dsum[:, n, :], scalar1=EPS, scalar2=None, op0=ALU.add)
            else:
                nc.vector.reciprocal(out=rden[:, n, :], in_=dse[:, n, :])

        def regroup_last(i):
            raw = raws[i]
            xg = xgp.tile([P, BG // HALF, PASSES, HALF * F, PACK], BF16, name="xg", align_bytes=64)
            xgs[i] = xg
            for h in range(BG // HALF):
                for c in range(PASSES):
                    nc.vector.tensor_copy(
                        out=xg[:, h, c].rearrange("p (b g i) j -> p b g j i", b=HALF, i=8),
                        in_=raw[:, c, h * HALF:(h + 1) * HALF].rearrange("p b (j g i) -> p b g j i", j=PACK, i=8),
                    )

        def quant_last(i):
            xg = xgs[i]
            xc = xcp.tile([P, BG // HALF, PASSES, HALF * F], U32, name="xc", align_bytes=64)
            xs = xcp.tile([P, BG // HALF, PASSES, HALF * F], U8, name="xs", align_bytes=64)
            for h in range(BG // HALF):
                nc.vector.quantize_mx(
                    out=xc[:, h].rearrange("p c w -> p (c w)").bitcast(FP8X4),
                    scales=xs[:, h].rearrange("p c w -> p (c w)"),
                    in_=xg[:, h].rearrange("p c w j -> p (c w j)"),
                )
            xqs[i] = (xc, xs)

        def multiply_last(i):
            n, g = divmod(i, NG)
            xc, xs = xqs[i]
            o_sb = outp.tile([P, BG, MT, F], F32, name="o_sb")
            for h in range(BG // HALF):
                for mt in range(MT):
                    acc = accp.tile([P, HALF * F], F32, name="acc")
                    for c in range(PASSES):
                        nc.tensor.matmul_mx(
                            out=acc[:],
                            lhsT=a_codes[n][:, c, mt * P:(mt + 1) * P].bitcast(FP8X4),
                            lhsT_scale=a_scales[n][:, c, mt * P:(mt + 1) * P],
                            rhs=xc[:, h, c, :].bitcast(FP8X4),
                            rhs_scale=xs[:, h, c, :],
                            start=(c == 0), stop=(c == PASSES - 1),
                        )
                    evacuate(mt % 2 == 1, o_sb[:, h * HALF:(h + 1) * HALF, mt, :],
                             acc[:].rearrange("p (b f) -> p b f", f=F), n, mt)
                store(i, o_sb, h * HALF, HALF)

        def quant(i):
            xg = xgs[i]
            xc = xcp.tile([P, PASSES, COLS], U32, name="xc", align_bytes=64)
            xs = xcp.tile([P, PASSES, COLS], U8, name="xs", align_bytes=64)
            nc.vector.quantize_mx(
                out=xc[:].rearrange("p c w -> p (c w)").bitcast(FP8X4),
                scales=xs[:].rearrange("p c w -> p (c w)"),
                in_=xg[:].rearrange("p c w j -> p (c w j)"),
            )
            xqs[i] = (xc, xs)

        def evacuate(on_vector, dst, src, n, mt):
            if on_vector:
                nc.vector.tensor_scalar(out=dst, in0=src, scalar1=rden[:, n, mt:mt + 1], scalar2=None, op0=ALU.mult)
            else:
                nc.scalar.activation(out=dst, in_=src, func=ACT.Copy, scale=rden[:, n, mt:mt + 1])

        def store(i, o_sb, lo, count):
            n, g = divmod(i, NG)
            b0 = g * BG + lo
            nc.sync.dma_start(
                out=out[b0:b0 + count, n, :, :].rearrange("b (p m) f -> p b (m f)", m=MT),
                in_=o_sb[:, lo:lo + count].rearrange("p b m f -> p b (m f)"),
            )

        def multiply(i):
            n, g = divmod(i, NG)
            xc, xs = xqs[i]
            o_sb = outp.tile([P, BG, MT, F], F32, name="o_sb")
            for mt in range(MT):
                acc = accp.tile([P, COLS], F32, name="acc")
                for c in range(PASSES):
                    nc.tensor.matmul_mx(
                        out=acc[:],
                        lhsT=a_codes[n][:, c, mt * P:(mt + 1) * P].bitcast(FP8X4),
                        lhsT_scale=a_scales[n][:, c, mt * P:(mt + 1) * P],
                        rhs=xc[:, c, :].bitcast(FP8X4),
                        rhs_scale=xs[:, c, :],
                        start=(c == 0), stop=(c == PASSES - 1),
                    )
                evacuate(False, o_sb[:, :, mt, :],
                         acc[:].rearrange("p (b f) -> p b f", f=F), n, mt)
            store(i, o_sb, 0, BG)

        ahead = {-7: [(regroup_pass, 0, 0), (regroup_pass, 0, 1)]}
        behind = {
            -7: [(regroup_pass, 1, 0), (quant, 0)],
            -6: [(regroup_pass, 1, 1)],
            -5: [(regroup_pass, 2, 0), (quant, 1)],
            -4: [(regroup_pass, 2, 1)],
        }
        done_r = {0, 1, 2}
        done_q = {0, 1}

        def do_regroup(i):
            if 0 <= i < CHUNKS and i not in done_r:
                done_r.add(i)
                if i == CHUNKS - 1:
                    regroup_last(i)
                elif i == SHARED:
                    regroup_pass(i, 1)
                else:
                    regroup(i)

        def do_quant(i):
            if 0 <= i < CHUNKS and i not in done_q:
                done_q.add(i)
                if i == CHUNKS - 1:
                    quant_last(i)
                else:
                    quant(i)

        for p in range(-SIG_LEAD, CHUNKS):
            if RAW_BUFS <= p + LOAD_LEAD < CHUNKS:
                load(p + LOAD_LEAD)
            q = p + PROD_LEAD
            qt = p + TURN_LEAD
            if 0 <= qt < PIECES:
                turn(qt)
            if 0 <= p + SIG_LEAD < PIECES:
                sig(p + SIG_LEAD)
            if 0 <= qt < PIECES:
                take(qt)
            if p == CHUNKS - 1:
                multiply_last(p)
            elif p >= 0:
                multiply(p)
            if p + SHARED_LEAD == SHARED:
                regroup_on_scalar(SHARED, 0)
            r_due = 0 <= qt < PIECES and qt % MT == MT - 1
            if r_due:
                rden_step(qt // MT, 0)
            for work in ahead.get(p, []):
                work[0](*work[1:])
            if 0 <= q < PIECES:
                prod(q)
            for work in behind.get(p, []):
                work[0](*work[1:])
            if r_due:
                rden_step(qt // MT, 1)
            do_quant(p + XQ_LEAD)
            do_regroup(p + XR_LEAD)
            if r_due:
                qa(qt // MT)
